import numpy as np
import ml_dtypes


def mxq(x, axis, fmt="e4m3"):
    dtype, down = {"e4m3": (ml_dtypes.float8_e4m3fn, 7), "e5m2": (ml_dtypes.float8_e5m2, 14)}[fmt]
    v = np.moveaxis(np.asarray(x, np.float32).astype(ml_dtypes.bfloat16).astype(np.float64), axis, -1)
    blocks = v.reshape(v.shape[:-1] + (-1, 32))
    amax = np.abs(blocks).max(-1, keepdims=True)
    byte = np.maximum(np.where(amax > 0, np.frexp(amax)[1] - 1 + 127, 0) - down, 1)
    scale = np.exp2(byte - 127.0)
    codes = (blocks / scale).astype(np.float32).astype(dtype).astype(np.float64)
    return np.moveaxis((codes * scale).reshape(v.shape), -1, axis)


WIDE = False


def mx_kscale(k):
    if not WIDE:
        return np.ones(k)
    levels = np.array([10, -10, 5, -5, 0])
    a = np.random.permutation(np.resize(levels, k // 512 * 4)).reshape(k // 512, 4)
    idx = np.arange(k)
    return np.exp2(a[idx // 512, idx % 128 // 32])


BF16 = ml_dtypes.bfloat16


def bf(x):
    return np.asarray(x, np.float32).astype(BF16)


def f64(x):
    return np.asarray(x).astype(np.float64)


B, C, H, W = 8, 256, 16, 32
HW = H * W


def softmax(z):
    e = np.exp(z - z.max(-1, keepdims=True))
    return e / e.sum(-1, keepdims=True)


def setup_inputs():
    s = mx_kscale(HW)
    return {"att": bf(np.random.standard_normal((B, HW, HW)) * 2.0 * np.sqrt(C / HW) * s),
            "v_spa": bf(np.random.standard_normal((B, C, HW)) * 3.0),
            "v_freq": bf(np.random.standard_normal((B, C, HW)) * 3.0),
            "x_spa": bf(np.random.standard_normal((B, C, H, W))),
            "x_freq": bf(np.random.standard_normal((B, C, H, W))),
            "w_spa": bf(np.random.standard_normal((HW, HW)) * np.sqrt(2.0 / HW) / s[None, :]),
            "b_spa": bf(np.random.standard_normal(HW) * 0.3),
            "w_frq": bf(np.random.standard_normal((HW, HW)) * np.sqrt(2.0 / HW) / s[None, :]),
            "b_frq": bf(np.random.standard_normal(HW) * 0.3)}


def reference(att, v_spa, v_freq, x_spa, x_freq, w_spa, b_spa, w_frq, b_frq):
    aq = mxq(f64(att), 2, "e4m3")
    p_spa = softmax((aq @ mxq(f64(w_spa), 1, "e4m3").T) + f64(b_spa))
    p_frq = softmax((aq @ mxq(f64(w_frq), 1, "e4m3").T) + f64(b_frq))
    o_spa = mxq(f64(v_spa), 2, "e4m3") @ mxq(p_spa, 1, "e4m3")
    o_frq = mxq(f64(v_freq), 2, "e4m3") @ mxq(p_frq, 1, "e4m3")
    out_spa = f64(x_spa) + o_spa.reshape(B, C, H, W)
    out_freq = f64(x_freq) + o_frq.reshape(B, C, H, W)
    return out_spa, out_freq

@@ -1,0 +1,191 @@
+from contextlib import ExitStack
+
+import concourse.mybir as mybir
+from concourse.masks import make_identity
+
+F32 = mybir.dt.float32
+BF16 = mybir.dt.bfloat16
+U32 = mybir.dt.uint32
+U8 = mybir.dt.uint8
+FP8X4 = mybir.dt.float8_e4m3fn_x4
+ADD = mybir.AluOpType.add
+MAX = mybir.AluOpType.max
+EXP = mybir.ActivationFunctionType.Exp
+COPY = mybir.ActivationFunctionType.Copy
+
+P = 128
+PACK = 4
+B = 8
+C = 256
+HW = 512
+ROW_TILES = HW // P
+C_TILES = C // P
+WORDS = HW // 2
+
+FLOPS = 2 * B * 2 * (HW * HW * HW + C * HW * HW)
+
+
+def transpose_to_k_on_partitions(nc, psum, grouped, rows, ident, tiles):
+    row_words = rows[:].bitcast(F32)
+    grouped_words = grouped[:].bitcast(F32)
+    for pair in range(tiles // 2):
+        bank = psum.tile([P, 4 * P], F32, tag="tr")
+        for j in range(4):
+            col = (4 * pair + j) * P
+            nc.tensor.transpose(bank[:, j * P : (j + 1) * P], row_words[:, col : col + P], ident[:])
+        nc.scalar.copy(
+            out=grouped_words[:, 4 * pair * P : 4 * (pair + 1) * P].rearrange("p (t r u) -> p t r u", t=2, u=2),
+            in_=bank[:].rearrange("p (t u r) -> p t r u", t=2, u=2),
+        )
+
+
+def tile_cmia_pb_t_kernel(
+    tc, att, v_spa, v_freq, x_spa, x_freq, w_spa, b_spa, w_frq, b_frq, out_0, out_1
+):
+    nc = tc.nc
+    values = [v_spa, v_freq]
+    residuals = [x_spa, x_freq]
+    weights = [w_spa, w_frq]
+    biases = [b_spa, b_frq]
+    outs = [out_0, out_1]
+
+    with ExitStack() as ctx:
+        const = ctx.enter_context(tc.tile_pool(name="const", bufs=1))
+        loads = ctx.enter_context(tc.tile_pool(name="loads", bufs=3))
+        work = ctx.enter_context(tc.tile_pool(name="work", bufs=2))
+        soft = ctx.enter_context(tc.tile_pool(name="soft", bufs=3))
+        stats = ctx.enter_context(tc.tile_pool(name="stats", bufs=4))
+        psum_t = ctx.enter_context(tc.psum_pool(name="psum_t", bufs=2))
+        psum_z = ctx.enter_context(tc.psum_pool(name="psum_z", bufs=4))
+        psum_o = ctx.enter_context(tc.psum_pool(name="psum_o", bufs=2))
+
+        ident = const.tile([P, P], F32, name="ident")
+        make_identity(nc, ident[:])
+
+        w_codes = []
+        w_scales = []
+        bias_rows = []
+        for s in range(2):
+            w_rows = const.tile([P, ROW_TILES * HW], BF16, name="w_rows%d" % s)
+            nc.sync.dma_start(
+                out=w_rows[:].rearrange("p (t k) -> p t k", t=ROW_TILES),
+                in_=weights[s].rearrange("(t p) k -> p t k", p=P),
+            )
+            w_grouped = const.tile([P, HW * PACK], BF16, name="w_grouped%d" % s, align_bytes=64)
+            transpose_to_k_on_partitions(nc, psum_t, w_grouped, w_rows, ident, ROW_TILES)
+            codes = const.tile([P, HW], U32, name="w_codes%d" % s, align_bytes=64)
+            scales = const.tile([P, HW], U8, name="w_scales%d" % s, align_bytes=64)
+            nc.vector.quantize_mx(out=codes[:].bitcast(FP8X4), scales=scales[:], in_=w_grouped[:])
+            w_codes.append(codes)
+            w_scales.append(scales)
+            bias = const.tile([P, HW], BF16, name="bias%d" % s)
+            nc.sync.dma_start(out=bias[:], in_=biases[s].partition_broadcast(P))
+            bias_rows.append(bias)
+
+        for b in range(B):
+            att_rows = loads.tile([P, ROW_TILES * HW], BF16)
+            nc.sync.dma_start(
+                out=att_rows[:].rearrange("p (u e k) -> p u e k", u=2, e=2),
+                in_=att[b].rearrange("(u p e) k -> p u e k", u=2, e=2),
+            )
+            v_rows = loads.tile([P, 2 * C_TILES * HW], BF16)
+            x_rows = loads.tile([P, 2 * C_TILES * HW], BF16)
+            for s in range(2):
+                nc.sync.dma_start(
+                    out=v_rows[:, s * C_TILES * HW : (s + 1) * C_TILES * HW].rearrange("p (t n) -> p t n", t=C_TILES),
+                    in_=values[s][b].rearrange("(t p) n -> p t n", p=P),
+                )
+            for s in range(2):
+                nc.sync.dma_start(
+                    out=x_rows[:, s * C_TILES * HW : (s + 1) * C_TILES * HW].rearrange("p (t m) -> p t m", t=C_TILES),
+                    in_=residuals[s][b].rearrange("(t p) h w -> p t (h w)", p=P),
+                )
+
+            att_grouped = work.tile([P, HW * PACK], BF16, align_bytes=64)
+            transpose_to_k_on_partitions(nc, psum_t, att_grouped, att_rows, ident, ROW_TILES)
+            att_codes = work.tile([P, HW], U32, align_bytes=64)
+            att_scales = work.tile([P, HW], U8, align_bytes=64)
+            nc.vector.quantize_mx(out=att_codes[:].bitcast(FP8X4), scales=att_scales[:], in_=att_grouped[:])
+
+            v_grouped = work.tile([P, 2 * C * PACK], BF16, align_bytes=64)
+            transpose_to_k_on_partitions(nc, psum_t, v_grouped, v_rows, ident, 2 * C_TILES)
+            v_codes = work.tile([P, 2 * C], U32, align_bytes=64)
+            v_scales = work.tile([P, 2 * C], U8, align_bytes=64)
+            nc.vector.quantize_mx(out=v_codes[:].bitcast(FP8X4), scales=v_scales[:], in_=v_grouped[:])
+
+            for s in range(2):
+                logits = soft.tile([P, ROW_TILES * HW], F32)
+                for t in range(ROW_TILES):
+                    z = psum_z.tile([P, HW], F32)
+                    nc.tensor.matmul_mx(
+                        out=z[:],
+                        lhsT=att_codes[:, t * P : (t + 1) * P].bitcast(FP8X4),
+                        lhsT_scale=att_scales[:, t * P : (t + 1) * P],
+                        rhs=w_codes[s][:].bitcast(FP8X4),
+                        rhs_scale=w_scales[s][:],
+                        start=True,
+                        stop=True,
+                    )
+                    nc.vector.tensor_tensor(
+                        out=logits[:, t * HW : (t + 1) * HW], in0=z[:], in1=bias_rows[s][:], op=ADD
+                    )
+                neg_max = stats.tile([P, ROW_TILES], F32)
+                nc.vector.tensor_reduce(
+                    out=neg_max[:],
+                    in_=logits[:].rearrange("p (t m) -> p t m", t=ROW_TILES),
+                    axis=mybir.AxisListType.X,
+                    op=MAX,
+                    negate=True,
+                )
+                sums = stats.tile([P, ROW_TILES], F32)
+                for t in range(ROW_TILES):
+                    nc.scalar.activation(
+                        out=logits[:, t * HW : (t + 1) * HW],
+                        in_=logits[:, t * HW : (t + 1) * HW],
+                        func=EXP,
+                        bias=neg_max[:, t : t + 1],
+                        scale=1.0,
+                        accum_out=sums[:, t : t + 1],
+                    )
+                inv_sums = stats.tile([P, ROW_TILES], F32)
+                nc.vector.reciprocal(out=inv_sums[:], in_=sums[:])
+                probs = work.tile([P, ROW_TILES * HW], BF16)
+                for t in range(ROW_TILES):
+                    nc.scalar.activation(
+                        out=probs[:, t * HW : (t + 1) * HW],
+                        in_=logits[:, t * HW : (t + 1) * HW],
+                        func=COPY,
+                        scale=inv_sums[:, t : t + 1],
+                    )
+                p_grouped = work.tile([P, HW * PACK], BF16, align_bytes=64)
+                nc.vector.tensor_copy(
+                    out=p_grouped[:].rearrange("p (c i t) -> p c t i", i=4, t=PACK),
+                    in_=probs[:].rearrange("p (t c i) -> p c t i", t=PACK, i=4),
+                )
+                p_codes = work.tile([P, HW], U32, align_bytes=64)
+                p_scales = work.tile([P, HW], U8, align_bytes=64)
+                nc.vector.quantize_mx(out=p_codes[:].bitcast(FP8X4), scales=p_scales[:], in_=p_grouped[:])
+
+                result = soft.tile([P, C_TILES * HW], F32)
+                for ct in range(C_TILES):
+                    col = (s * C_TILES + ct) * P
+                    o = psum_o.tile([P, HW], F32)
+                    nc.tensor.matmul_mx(
+                        out=o[:],
+                        lhsT=v_codes[:, col : col + P].bitcast(FP8X4),
+                        lhsT_scale=v_scales[:, col : col + P],
+                        rhs=p_codes[:].bitcast(FP8X4),
+                        rhs_scale=p_scales[:],
+                        start=True,
+                        stop=True,
+                    )
+                    nc.vector.tensor_tensor(
+                        out=result[:, ct * HW : (ct + 1) * HW],
+                        in0=o[:],
+                        in1=x_rows[:, (s * C_TILES + ct) * HW : (s * C_TILES + ct + 1) * HW],
+                        op=ADD,
+                    )
+                nc.sync.dma_start(
+                    out=outs[s][b].rearrange("(t p) h w -> p t (h w)", p=P),
+                    in_=result[:].rearrange("p (t m) -> p t m", t=C_TILES),
+                )

@@ -10,8 +10,8 @@ U8 = mybir.dt.uint8
 FP8X4 = mybir.dt.float8_e4m3fn_x4
 ADD = mybir.AluOpType.add
 MAX = mybir.AluOpType.max
+MULT = mybir.AluOpType.mult
 EXP = mybir.ActivationFunctionType.Exp
-COPY = mybir.ActivationFunctionType.Copy
 
 P = 128
 PACK = 4
@@ -151,14 +151,16 @@ def tile_cmia_pb_t_kernel(
                 nc.vector.reciprocal(out=inv_sums[:], in_=sums[:])
                 probs = work.tile([P, ROW_TILES * HW], BF16)
                 for t in range(ROW_TILES):
-                    nc.scalar.activation(
+                    nc.gpsimd.tensor_scalar(
                         out=probs[:, t * HW : (t + 1) * HW],
-                        in_=logits[:, t * HW : (t + 1) * HW],
-                        func=COPY,
-                        scale=inv_sums[:, t : t + 1],
+                        in0=logits[:, t * HW : (t + 1) * HW],
+                        scalar1=inv_sums[:, t : t + 1],
+                        scalar2=0.0,
+                        op0=MULT,
+                        op1=ADD,
                     )
                 p_grouped = work.tile([P, HW * PACK], BF16, align_bytes=64)
-                nc.vector.tensor_copy(
+                nc.scalar.copy(
                     out=p_grouped[:].rearrange("p (c i t) -> p c t i", i=4, t=PACK),
                     in_=probs[:].rearrange("p (t c i) -> p c t i", t=PACK, i=4),
                 )

@@ -12,6 +12,7 @@ ADD = mybir.AluOpType.add
 MAX = mybir.AluOpType.max
 MULT = mybir.AluOpType.mult
 EXP = mybir.ActivationFunctionType.Exp
+COPY = mybir.ActivationFunctionType.Copy
 
 P = 128
 PACK = 4
@@ -21,6 +22,8 @@ HW = 512
 ROW_TILES = HW // P
 C_TILES = C // P
 WORDS = HW // 2
+
+REGROUP_PIECES = 4
 
 FLOPS = 2 * B * 2 * (HW * HW * HW + C * HW * HW)
 
@@ -52,54 +55,75 @@ def tile_cmia_pb_t_kernel(
     with ExitStack() as ctx:
         const = ctx.enter_context(tc.tile_pool(name="const", bufs=1))
         loads = ctx.enter_context(tc.tile_pool(name="loads", bufs=3))
-        work = ctx.enter_context(tc.tile_pool(name="work", bufs=2))
+        work = ctx.enter_context(tc.tile_pool(name="work", bufs=3))
         soft = ctx.enter_context(tc.tile_pool(name="soft", bufs=3))
         stats = ctx.enter_context(tc.tile_pool(name="stats", bufs=4))
         psum_t = ctx.enter_context(tc.psum_pool(name="psum_t", bufs=2))
         psum_z = ctx.enter_context(tc.psum_pool(name="psum_z", bufs=4))
         psum_o = ctx.enter_context(tc.psum_pool(name="psum_o", bufs=2))
 
-        ident = const.tile([P, P], F32, name="ident")
-        make_identity(nc, ident[:])
-
-        w_codes = []
-        w_scales = []
-        bias_rows = []
-        for s in range(2):
+        def load_weight(s):
             w_rows = const.tile([P, ROW_TILES * HW], BF16, name="w_rows%d" % s)
             nc.sync.dma_start(
                 out=w_rows[:].rearrange("p (t k) -> p t k", t=ROW_TILES),
                 in_=weights[s].rearrange("(t p) k -> p t k", p=P),
             )
+            return w_rows
+
+        def load_sample(b):
+            att_rows = loads.tile([P, ROW_TILES * HW], BF16, name="att_rows")
+            nc.sync.dma_start(
+                out=att_rows[:].rearrange("p (u e k) -> p u e k", u=2, e=2),
+                in_=att[b].rearrange("(u p e) k -> p u e k", u=2, e=2),
+            )
+            v_rows = loads.tile([P, 2 * C_TILES * HW], BF16, name="v_rows")
+            x_rows = loads.tile([P, 2 * C_TILES * HW], BF16, name="x_rows")
+            for s in range(2):
+                nc.sync.dma_start(
+                    out=v_rows[:, s * C_TILES * HW : (s + 1) * C_TILES * HW],
+                    in_=values[s][b].rearrange("(p t) n -> p (t n)", t=C_TILES),
+                )
+            for s in range(2):
+                nc.sync.dma_start(
+                    out=x_rows[:, s * C_TILES * HW : (s + 1) * C_TILES * HW],
+                    in_=residuals[s][b].rearrange("(p t) h w -> p (t h w)", t=C_TILES),
+                )
+            return att_rows, v_rows, x_rows
+
+        bias_in = const.tile([P, 2 * HW], BF16, name="bias_in")
+        nc.vector.memset(bias_in[:].bitcast(mybir.dt.int32), 0)
+        for s in range(2):
+            nc.scalar.dma_start(out=bias_in[0:1, s * HW : (s + 1) * HW], in_=biases[s].unsqueeze(0))
+        w_rows = [load_weight(0)]
+        next_sample = load_sample(0)
+        w_rows.append(load_weight(1))
+
+        ident = const.tile([P, P], F32, name="ident")
+        make_identity(nc, ident[:])
+        ones = const.tile([P, P], BF16, name="ones")
+        nc.vector.memset(ones[:], 1.0)
+
+        w_codes = []
+        w_scales = []
+        bias_rows = []
+        for s in range(2):
             w_grouped = const.tile([P, HW * PACK], BF16, name="w_grouped%d" % s, align_bytes=64)
-            transpose_to_k_on_partitions(nc, psum_t, w_grouped, w_rows, ident, ROW_TILES)
+            transpose_to_k_on_partitions(nc, psum_t, w_grouped, w_rows[s], ident, ROW_TILES)
             codes = const.tile([P, HW], U32, name="w_codes%d" % s, align_bytes=64)
             scales = const.tile([P, HW], U8, name="w_scales%d" % s, align_bytes=64)
             nc.vector.quantize_mx(out=codes[:].bitcast(FP8X4), scales=scales[:], in_=w_grouped[:])
             w_codes.append(codes)
             w_scales.append(scales)
-            bias = const.tile([P, HW], BF16, name="bias%d" % s)
-            nc.sync.dma_start(out=bias[:], in_=biases[s].partition_broadcast(P))
+            spread = psum_z.tile([P, HW], F32, tag="z")
+            nc.tensor.matmul(out=spread[:], lhsT=ones[:], rhs=bias_in[:, s * HW : (s + 1) * HW], start=True, stop=True)
+            bias = const.tile([P, HW], F32, name="bias%d" % s)
+            nc.vector.tensor_copy(out=bias[:], in_=spread[:])
             bias_rows.append(bias)
 
         for b in range(B):
-            att_rows = loads.tile([P, ROW_TILES * HW], BF16)
-            nc.sync.dma_start(
-                out=att_rows[:].rearrange("p (u e k) -> p u e k", u=2, e=2),
-                in_=att[b].rearrange("(u p e) k -> p u e k", u=2, e=2),
-            )
-            v_rows = loads.tile([P, 2 * C_TILES * HW], BF16)
-            x_rows = loads.tile([P, 2 * C_TILES * HW], BF16)
-            for s in range(2):
-                nc.sync.dma_start(
-                    out=v_rows[:, s * C_TILES * HW : (s + 1) * C_TILES * HW].rearrange("p (t n) -> p t n", t=C_TILES),
-                    in_=values[s][b].rearrange("(t p) n -> p t n", p=P),
-                )
-            for s in range(2):
-                nc.sync.dma_start(
-                    out=x_rows[:, s * C_TILES * HW : (s + 1) * C_TILES * HW].rearrange("p (t m) -> p t m", t=C_TILES),
-                    in_=residuals[s][b].rearrange("(t p) h w -> p t (h w)", p=P),
-                )
+            att_rows, v_rows, x_rows = next_sample
+            if b + 1 < B:
+                next_sample = load_sample(b + 1)
 
             att_grouped = work.tile([P, HW * PACK], BF16, align_bytes=64)
             transpose_to_k_on_partitions(nc, psum_t, att_grouped, att_rows, ident, ROW_TILES)
@@ -116,7 +140,7 @@ def tile_cmia_pb_t_kernel(
             for s in range(2):
                 logits = soft.tile([P, ROW_TILES * HW], F32)
                 for t in range(ROW_TILES):
-                    z = psum_z.tile([P, HW], F32)
+                    z = psum_z.tile([P, HW], F32, tag="z")
                     nc.tensor.matmul_mx(
                         out=z[:],
                         lhsT=att_codes[:, t * P : (t + 1) * P].bitcast(FP8X4),
@@ -151,19 +175,25 @@ def tile_cmia_pb_t_kernel(
                 nc.vector.reciprocal(out=inv_sums[:], in_=sums[:])
                 probs = work.tile([P, ROW_TILES * HW], BF16)
                 for t in range(ROW_TILES):
-                    nc.gpsimd.tensor_scalar(
+                    nc.scalar.activation(
                         out=probs[:, t * HW : (t + 1) * HW],
-                        in0=logits[:, t * HW : (t + 1) * HW],
-                        scalar1=inv_sums[:, t : t + 1],
+                        in_=logits[:, t * HW : (t + 1) * HW],
+                        func=COPY,
+                        scale=inv_sums[:, t : t + 1],
+                    )
+                p_grouped = work.tile([P, HW * PACK], BF16, align_bytes=64)
+                probs_by_column = probs[:].rearrange("p (t m) -> p m t", t=PACK)
+                for piece in range(REGROUP_PIECES):
+                    m0 = piece * (HW // REGROUP_PIECES)
+                    m1 = m0 + HW // REGROUP_PIECES
+                    nc.gpsimd.tensor_scalar(
+                        out=p_grouped[:, m0 * PACK : m1 * PACK].rearrange("p (m t) -> p m t", t=PACK),
+                        in0=probs_by_column[:, m0:m1, :],
+                        scalar1=1.0,
                         scalar2=0.0,
                         op0=MULT,
                         op1=ADD,
                     )
-                p_grouped = work.tile([P, HW * PACK], BF16, align_bytes=64)
-                nc.scalar.copy(
-                    out=p_grouped[:].rearrange("p (c i t) -> p c t i", i=4, t=PACK),
-                    in_=probs[:].rearrange("p (t c i) -> p c t i", t=PACK, i=4),
-                )
                 p_codes = work.tile([P, HW], U32, align_bytes=64)
                 p_scales = work.tile([P, HW], U8, align_bytes=64)
                 nc.vector.quantize_mx(out=p_codes[:].bitcast(FP8X4), scales=p_scales[:], in_=p_grouped[:])
@@ -187,7 +217,4 @@ def tile_cmia_pb_t_kernel(
                         in1=x_rows[:, (s * C_TILES + ct) * HW : (s * C_TILES + ct + 1) * HW],
                         op=ADD,
                     )
-                nc.sync.dma_start(
-                    out=outs[s][b].rearrange("(t p) h w -> p t (h w)", p=P),
-                    in_=result[:].rearrange("p (t m) -> p t m", t=C_TILES),
-                )
+                nc.sync.dma_start(out=outs[s][b].rearrange("(p t) h w -> p (t h w)", t=C_TILES), in_=result[:])

@@ -12,7 +12,6 @@ ADD = mybir.AluOpType.add
 MAX = mybir.AluOpType.max
 MULT = mybir.AluOpType.mult
 EXP = mybir.ActivationFunctionType.Exp
-COPY = mybir.ActivationFunctionType.Copy
 
 P = 128
 PACK = 4
@@ -56,7 +55,7 @@ def tile_cmia_pb_t_kernel(
         const = ctx.enter_context(tc.tile_pool(name="const", bufs=1))
         loads = ctx.enter_context(tc.tile_pool(name="loads", bufs=3))
         work = ctx.enter_context(tc.tile_pool(name="work", bufs=3))
-        soft = ctx.enter_context(tc.tile_pool(name="soft", bufs=3))
+        soft = ctx.enter_context(tc.tile_pool(name="soft", bufs=4))
         stats = ctx.enter_context(tc.tile_pool(name="stats", bufs=4))
         psum_t = ctx.enter_context(tc.psum_pool(name="psum_t", bufs=2))
         psum_z = ctx.enter_context(tc.psum_pool(name="psum_z", bufs=4))
@@ -173,26 +172,16 @@ def tile_cmia_pb_t_kernel(
                     )
                 inv_sums = stats.tile([P, ROW_TILES], F32)
                 nc.vector.reciprocal(out=inv_sums[:], in_=sums[:])
-                probs = work.tile([P, ROW_TILES * HW], BF16)
-                for t in range(ROW_TILES):
-                    nc.scalar.activation(
-                        out=probs[:, t * HW : (t + 1) * HW],
-                        in_=logits[:, t * HW : (t + 1) * HW],
-                        func=COPY,
-                        scale=inv_sums[:, t : t + 1],
-                    )
                 p_grouped = work.tile([P, HW * PACK], BF16, align_bytes=64)
-                probs_by_column = probs[:].rearrange("p (t m) -> p m t", t=PACK)
+                exps_by_column = logits[:].rearrange("p (t m) -> p m t", t=PACK)
+                piece_cols = HW // REGROUP_PIECES
                 for piece in range(REGROUP_PIECES):
-                    m0 = piece * (HW // REGROUP_PIECES)
-                    m1 = m0 + HW // REGROUP_PIECES
-                    nc.gpsimd.tensor_scalar(
-                        out=p_grouped[:, m0 * PACK : m1 * PACK].rearrange("p (m t) -> p m t", t=PACK),
-                        in0=probs_by_column[:, m0:m1, :],
-                        scalar1=1.0,
-                        scalar2=0.0,
-                        op0=MULT,
-                        op1=ADD,
+                    m0 = piece * piece_cols
+                    nc.gpsimd.tensor_tensor(
+                        out=p_grouped[:, m0 * PACK : (m0 + piece_cols) * PACK].rearrange("p (m t) -> p m t", t=PACK),
+                        in0=exps_by_column[:, m0 : m0 + piece_cols, :],
+                        in1=inv_sums[:].unsqueeze(1).to_broadcast([P, piece_cols, PACK]),
+                        op=MULT,
                     )
                 p_codes = work.tile([P, HW], U32, align_bytes=64)
                 p_scales = work.tile([P, HW], U8, align_bytes=64)

@@ -5,6 +5,7 @@ from concourse.masks import make_identity
 
 F32 = mybir.dt.float32
 BF16 = mybir.dt.bfloat16
+I32 = mybir.dt.int32
 U32 = mybir.dt.uint32
 U8 = mybir.dt.uint8
 FP8X4 = mybir.dt.float8_e4m3fn_x4
@@ -12,6 +13,7 @@ ADD = mybir.AluOpType.add
 MAX = mybir.AluOpType.max
 MULT = mybir.AluOpType.mult
 EXP = mybir.ActivationFunctionType.Exp
+COPY = mybir.ActivationFunctionType.Copy
 
 P = 128
 PACK = 4
@@ -20,25 +22,11 @@ C = 256
 HW = 512
 ROW_TILES = HW // P
 C_TILES = C // P
-WORDS = HW // 2
-
+UNITS = 2 * B
 REGROUP_PIECES = 4
+LOAD_AHEAD = 3
 
 FLOPS = 2 * B * 2 * (HW * HW * HW + C * HW * HW)
-
-
-def transpose_to_k_on_partitions(nc, psum, grouped, rows, ident, tiles):
-    row_words = rows[:].bitcast(F32)
-    grouped_words = grouped[:].bitcast(F32)
-    for pair in range(tiles // 2):
-        bank = psum.tile([P, 4 * P], F32, tag="tr")
-        for j in range(4):
-            col = (4 * pair + j) * P
-            nc.tensor.transpose(bank[:, j * P : (j + 1) * P], row_words[:, col : col + P], ident[:])
-        nc.scalar.copy(
-            out=grouped_words[:, 4 * pair * P : 4 * (pair + 1) * P].rearrange("p (t r u) -> p t r u", t=2, u=2),
-            in_=bank[:].rearrange("p (t u r) -> p t r u", t=2, u=2),
-        )
 
 
 def tile_cmia_pb_t_kernel(
@@ -51,159 +39,242 @@ def tile_cmia_pb_t_kernel(
     biases = [b_spa, b_frq]
     outs = [out_0, out_1]
 
+    operands = [("w", 0), ("att", 0), ("w", 1), ("v", 0)]
+    for b in range(1, B):
+        operands.extend([("att", b), ("v", b)])
+
     with ExitStack() as ctx:
+        ctx.enter_context(tc.manual_schedule())
         const = ctx.enter_context(tc.tile_pool(name="const", bufs=1))
         loads = ctx.enter_context(tc.tile_pool(name="loads", bufs=3))
-        work = ctx.enter_context(tc.tile_pool(name="work", bufs=3))
-        soft = ctx.enter_context(tc.tile_pool(name="soft", bufs=4))
+        late_loads = ctx.enter_context(tc.tile_pool(name="late_loads", bufs=5))
+        packed = ctx.enter_context(tc.tile_pool(name="packed", bufs=5))
+        work = ctx.enter_context(tc.tile_pool(name="work", bufs=2))
+        soft = ctx.enter_context(tc.tile_pool(name="soft", bufs=3))
         stats = ctx.enter_context(tc.tile_pool(name="stats", bufs=4))
         psum_t = ctx.enter_context(tc.psum_pool(name="psum_t", bufs=2))
         psum_z = ctx.enter_context(tc.psum_pool(name="psum_z", bufs=4))
         psum_o = ctx.enter_context(tc.psum_pool(name="psum_o", bufs=2))
 
+        rows = {}
+        x_rows = {}
+        banks = {}
+        grouped = {}
+        codes = {}
+        scales = {}
+        z_banks = {}
+        logits = {}
+        neg_max = {}
+        sums = {}
+        probs = {}
+        p_grouped = {}
+        o_banks = {}
+
         def load_weight(s):
-            w_rows = const.tile([P, ROW_TILES * HW], BF16, name="w_rows%d" % s)
+            rows[("w", s)] = const.tile([P, ROW_TILES * HW], BF16, name="w_rows%d" % s)
             nc.sync.dma_start(
-                out=w_rows[:].rearrange("p (t k) -> p t k", t=ROW_TILES),
+                out=rows[("w", s)][:].rearrange("p (t k) -> p t k", t=ROW_TILES),
                 in_=weights[s].rearrange("(t p) k -> p t k", p=P),
             )
-            return w_rows
 
-        def load_sample(b):
-            att_rows = loads.tile([P, ROW_TILES * HW], BF16, name="att_rows")
+        def load_att(b):
+            rows[("att", b)] = loads.tile([P, ROW_TILES * HW], BF16, name="att_rows")
             nc.sync.dma_start(
-                out=att_rows[:].rearrange("p (u e k) -> p u e k", u=2, e=2),
+                out=rows[("att", b)][:].rearrange("p (u e k) -> p u e k", u=2, e=2),
                 in_=att[b].rearrange("(u p e) k -> p u e k", u=2, e=2),
             )
-            v_rows = loads.tile([P, 2 * C_TILES * HW], BF16, name="v_rows")
-            x_rows = loads.tile([P, 2 * C_TILES * HW], BF16, name="x_rows")
+
+        def load_values_and_residuals(b):
+            rows[("v", b)] = loads.tile([P, 2 * C_TILES * HW], BF16, name="v_rows")
+            x_rows[b] = late_loads.tile([P, 2 * C_TILES * HW], BF16, name="x_rows")
             for s in range(2):
                 nc.sync.dma_start(
-                    out=v_rows[:, s * C_TILES * HW : (s + 1) * C_TILES * HW],
+                    out=rows[("v", b)][:, s * C_TILES * HW : (s + 1) * C_TILES * HW],
                     in_=values[s][b].rearrange("(p t) n -> p (t n)", t=C_TILES),
                 )
             for s in range(2):
                 nc.sync.dma_start(
-                    out=x_rows[:, s * C_TILES * HW : (s + 1) * C_TILES * HW],
+                    out=x_rows[b][:, s * C_TILES * HW : (s + 1) * C_TILES * HW],
                     in_=residuals[s][b].rearrange("(p t) h w -> p (t h w)", t=C_TILES),
                 )
-            return att_rows, v_rows, x_rows
+
+        def transpose_operand(op):
+            row_words = rows[op][:].bitcast(F32)
+            banks[op] = []
+            for pair in range(2):
+                bank = psum_t.tile([P, 4 * P], F32, name="tr")
+                for j in range(4):
+                    col = (4 * pair + j) * P
+                    nc.tensor.transpose(bank[:, j * P : (j + 1) * P], row_words[:, col : col + P], ident[:])
+                banks[op].append(bank)
+
+        def copy_operand_out(op):
+            grouped[op] = work.tile([P, HW * PACK], BF16, name="grouped", align_bytes=64)
+            grouped_words = grouped[op][:].bitcast(F32)
+            for pair in range(2):
+                nc.scalar.copy(
+                    out=grouped_words[:, 4 * pair * P : 4 * (pair + 1) * P].rearrange("p (t r u) -> p t r u", t=2, u=2),
+                    in_=banks[op][pair][:].rearrange("p (t u r) -> p t r u", t=2, u=2),
+                )
+
+        def quantise(key, pool, name, source):
+            codes[key] = pool.tile([P, HW], U32, name=name + "_codes", align_bytes=64)
+            scales[key] = pool.tile([P, HW], U8, name=name + "_scales", align_bytes=64)
+            nc.vector.quantize_mx(out=codes[key][:].bitcast(FP8X4), scales=scales[key][:], in_=source[:])
+
+        def quantise_operand(op):
+            if op[0] == "w":
+                quantise(op, const, "w%d" % op[1], grouped[op])
+            else:
+                quantise(op, packed, "operand", grouped[op])
+
+        def first_matmuls(unit):
+            b, s = divmod(unit, 2)
+            z_banks[unit] = []
+            for t in range(ROW_TILES):
+                z = psum_z.tile([P, HW], F32, name="z")
+                nc.tensor.matmul_mx(
+                    out=z[:],
+                    lhsT=codes[("att", b)][:, t * P : (t + 1) * P].bitcast(FP8X4),
+                    lhsT_scale=scales[("att", b)][:, t * P : (t + 1) * P],
+                    rhs=codes[("w", s)][:].bitcast(FP8X4),
+                    rhs_scale=scales[("w", s)][:],
+                    start=True,
+                    stop=True,
+                )
+                z_banks[unit].append(z)
+
+        def add_bias(unit):
+            logits[unit] = soft.tile([P, ROW_TILES * HW], F32, name="logits")
+            for t in range(ROW_TILES):
+                nc.vector.tensor_tensor(
+                    out=logits[unit][:, t * HW : (t + 1) * HW], in0=z_banks[unit][t][:], in1=bias_rows[unit % 2][:], op=ADD
+                )
+
+        def row_maxima(unit):
+            neg_max[unit] = stats.tile([P, ROW_TILES], F32, name="neg_max")
+            nc.vector.tensor_reduce(
+                out=neg_max[unit][:],
+                in_=logits[unit][:].rearrange("p (t m) -> p t m", t=ROW_TILES),
+                axis=mybir.AxisListType.X,
+                op=MAX,
+                negate=True,
+            )
+
+        def exponentials(unit):
+            sums[unit] = stats.tile([P, ROW_TILES], F32, name="sums")
+            for t in range(ROW_TILES):
+                nc.scalar.activation(
+                    out=logits[unit][:, t * HW : (t + 1) * HW],
+                    in_=logits[unit][:, t * HW : (t + 1) * HW],
+                    func=EXP,
+                    bias=neg_max[unit][:, t : t + 1],
+                    scale=1.0,
+                    accum_out=sums[unit][:, t : t + 1],
+                )
+
+        def normalise(unit):
+            inv_sums = stats.tile([P, ROW_TILES], F32, name="inv_sums")
+            nc.vector.reciprocal(out=inv_sums[:], in_=sums[unit][:])
+            probs[unit] = work.tile([P, ROW_TILES * HW], BF16, name="probs")
+            for t in range(ROW_TILES):
+                nc.scalar.activation(
+                    out=probs[unit][:, t * HW : (t + 1) * HW],
+                    in_=logits[unit][:, t * HW : (t + 1) * HW],
+                    func=COPY,
+                    scale=inv_sums[:, t : t + 1],
+                )
+
+        def regroup(unit):
+            p_grouped[unit] = work.tile([P, HW * PACK], BF16, name="p_grouped", align_bytes=64)
+            by_column = probs[unit][:].rearrange("p (t m) -> p m t", t=PACK)
+            piece_cols = HW // REGROUP_PIECES
+            for piece in range(REGROUP_PIECES):
+                m0 = piece * piece_cols
+                nc.gpsimd.tensor_scalar(
+                    out=p_grouped[unit][:, m0 * PACK : (m0 + piece_cols) * PACK].rearrange("p (m t) -> p m t", t=PACK),
+                    in0=by_column[:, m0 : m0 + piece_cols, :],
+                    scalar1=1.0,
+                    scalar2=0.0,
+                    op0=MULT,
+                    op1=ADD,
+                )
+
+        def second_matmuls(unit):
+            b, s = divmod(unit, 2)
+            o_banks[unit] = []
+            for ct in range(C_TILES):
+                col = (s * C_TILES + ct) * P
+                o = psum_o.tile([P, HW], F32, name="o")
+                nc.tensor.matmul_mx(
+                    out=o[:],
+                    lhsT=codes[("v", b)][:, col : col + P].bitcast(FP8X4),
+                    lhsT_scale=scales[("v", b)][:, col : col + P],
+                    rhs=codes[("p", unit)][:].bitcast(FP8X4),
+                    rhs_scale=scales[("p", unit)][:],
+                    start=True,
+                    stop=True,
+                )
+                o_banks[unit].append(o)
+
+        def add_residual_and_store(unit):
+            b, s = divmod(unit, 2)
+            result = soft.tile([P, C_TILES * HW], F32, name="result")
+            for ct in range(C_TILES):
+                nc.vector.tensor_tensor(
+                    out=result[:, ct * HW : (ct + 1) * HW],
+                    in0=o_banks[unit][ct][:],
+                    in1=x_rows[b][:, (s * C_TILES + ct) * HW : (s * C_TILES + ct + 1) * HW],
+                    op=ADD,
+                )
+            nc.sync.dma_start(out=outs[s][b].rearrange("(p t) h w -> p (t h w)", t=C_TILES), in_=result[:])
 
         bias_in = const.tile([P, 2 * HW], BF16, name="bias_in")
-        nc.vector.memset(bias_in[:].bitcast(mybir.dt.int32), 0)
-        for s in range(2):
-            nc.scalar.dma_start(out=bias_in[0:1, s * HW : (s + 1) * HW], in_=biases[s].unsqueeze(0))
-        w_rows = [load_weight(0)]
-        next_sample = load_sample(0)
-        w_rows.append(load_weight(1))
-
-        ident = const.tile([P, P], F32, name="ident")
-        make_identity(nc, ident[:])
+        nc.vector.memset(bias_in[:].bitcast(I32), 0)
         ones = const.tile([P, P], BF16, name="ones")
         nc.vector.memset(ones[:], 1.0)
+        ident = const.tile([P, P], F32, name="ident")
+        make_identity(nc, ident[:])
+        for s in range(2):
+            nc.scalar.dma_start(out=bias_in[0:1, s * HW : (s + 1) * HW], in_=biases[s].unsqueeze(0))
+        load_weight(0)
+        load_att(0)
+        load_weight(1)
+        load_values_and_residuals(0)
+        for b in range(1, LOAD_AHEAD):
+            load_att(b)
+            load_values_and_residuals(b)
 
-        w_codes = []
-        w_scales = []
         bias_rows = []
         for s in range(2):
-            w_grouped = const.tile([P, HW * PACK], BF16, name="w_grouped%d" % s, align_bytes=64)
-            transpose_to_k_on_partitions(nc, psum_t, w_grouped, w_rows[s], ident, ROW_TILES)
-            codes = const.tile([P, HW], U32, name="w_codes%d" % s, align_bytes=64)
-            scales = const.tile([P, HW], U8, name="w_scales%d" % s, align_bytes=64)
-            nc.vector.quantize_mx(out=codes[:].bitcast(FP8X4), scales=scales[:], in_=w_grouped[:])
-            w_codes.append(codes)
-            w_scales.append(scales)
-            spread = psum_z.tile([P, HW], F32, tag="z")
+            spread = psum_z.tile([P, HW], F32, name="z")
             nc.tensor.matmul(out=spread[:], lhsT=ones[:], rhs=bias_in[:, s * HW : (s + 1) * HW], start=True, stop=True)
             bias = const.tile([P, HW], F32, name="bias%d" % s)
             nc.vector.tensor_copy(out=bias[:], in_=spread[:])
             bias_rows.append(bias)
 
-        for b in range(B):
-            att_rows, v_rows, x_rows = next_sample
-            if b + 1 < B:
-                next_sample = load_sample(b + 1)
-
-            att_grouped = work.tile([P, HW * PACK], BF16, align_bytes=64)
-            transpose_to_k_on_partitions(nc, psum_t, att_grouped, att_rows, ident, ROW_TILES)
-            att_codes = work.tile([P, HW], U32, align_bytes=64)
-            att_scales = work.tile([P, HW], U8, align_bytes=64)
-            nc.vector.quantize_mx(out=att_codes[:].bitcast(FP8X4), scales=att_scales[:], in_=att_grouped[:])
-
-            v_grouped = work.tile([P, 2 * C * PACK], BF16, align_bytes=64)
-            transpose_to_k_on_partitions(nc, psum_t, v_grouped, v_rows, ident, 2 * C_TILES)
-            v_codes = work.tile([P, 2 * C], U32, align_bytes=64)
-            v_scales = work.tile([P, 2 * C], U8, align_bytes=64)
-            nc.vector.quantize_mx(out=v_codes[:].bitcast(FP8X4), scales=v_scales[:], in_=v_grouped[:])
-
-            for s in range(2):
-                logits = soft.tile([P, ROW_TILES * HW], F32)
-                for t in range(ROW_TILES):
-                    z = psum_z.tile([P, HW], F32, tag="z")
-                    nc.tensor.matmul_mx(
-                        out=z[:],
-                        lhsT=att_codes[:, t * P : (t + 1) * P].bitcast(FP8X4),
-                        lhsT_scale=att_scales[:, t * P : (t + 1) * P],
-                        rhs=w_codes[s][:].bitcast(FP8X4),
-                        rhs_scale=w_scales[s][:],
-                        start=True,
-                        stop=True,
-                    )
-                    nc.vector.tensor_tensor(
-                        out=logits[:, t * HW : (t + 1) * HW], in0=z[:], in1=bias_rows[s][:], op=ADD
-                    )
-                neg_max = stats.tile([P, ROW_TILES], F32)
-                nc.vector.tensor_reduce(
-                    out=neg_max[:],
-                    in_=logits[:].rearrange("p (t m) -> p t m", t=ROW_TILES),
-                    axis=mybir.AxisListType.X,
-                    op=MAX,
-                    negate=True,
-                )
-                sums = stats.tile([P, ROW_TILES], F32)
-                for t in range(ROW_TILES):
-                    nc.scalar.activation(
-                        out=logits[:, t * HW : (t + 1) * HW],
-                        in_=logits[:, t * HW : (t + 1) * HW],
-                        func=EXP,
-                        bias=neg_max[:, t : t + 1],
-                        scale=1.0,
-                        accum_out=sums[:, t : t + 1],
-                    )
-                inv_sums = stats.tile([P, ROW_TILES], F32)
-                nc.vector.reciprocal(out=inv_sums[:], in_=sums[:])
-                p_grouped = work.tile([P, HW * PACK], BF16, align_bytes=64)
-                exps_by_column = logits[:].rearrange("p (t m) -> p m t", t=PACK)
-                piece_cols = HW // REGROUP_PIECES
-                for piece in range(REGROUP_PIECES):
-                    m0 = piece * piece_cols
-                    nc.gpsimd.tensor_tensor(
-                        out=p_grouped[:, m0 * PACK : (m0 + piece_cols) * PACK].rearrange("p (m t) -> p m t", t=PACK),
-                        in0=exps_by_column[:, m0 : m0 + piece_cols, :],
-                        in1=inv_sums[:].unsqueeze(1).to_broadcast([P, piece_cols, PACK]),
-                        op=MULT,
-                    )
-                p_codes = work.tile([P, HW], U32, align_bytes=64)
-                p_scales = work.tile([P, HW], U8, align_bytes=64)
-                nc.vector.quantize_mx(out=p_codes[:].bitcast(FP8X4), scales=p_scales[:], in_=p_grouped[:])
-
-                result = soft.tile([P, C_TILES * HW], F32)
-                for ct in range(C_TILES):
-                    col = (s * C_TILES + ct) * P
-                    o = psum_o.tile([P, HW], F32)
-                    nc.tensor.matmul_mx(
-                        out=o[:],
-                        lhsT=v_codes[:, col : col + P].bitcast(FP8X4),
-                        lhsT_scale=v_scales[:, col : col + P],
-                        rhs=p_codes[:].bitcast(FP8X4),
-                        rhs_scale=p_scales[:],
-                        start=True,
-                        stop=True,
-                    )
-                    nc.vector.tensor_tensor(
-                        out=result[:, ct * HW : (ct + 1) * HW],
-                        in0=o[:],
-                        in1=x_rows[:, (s * C_TILES + ct) * HW : (s * C_TILES + ct + 1) * HW],
-                        op=ADD,
-                    )
-                nc.sync.dma_start(out=outs[s][b].rearrange("(p t) h w -> p (t h w)", t=C_TILES), in_=result[:])
+        for step in range(-5, UNITS + 2):
+            if step >= 0 and step % 2 == 0 and step // 2 + LOAD_AHEAD < B:
+                load_att(step // 2 + LOAD_AHEAD)
+                load_values_and_residuals(step // 2 + LOAD_AHEAD)
+            if 0 <= step < UNITS:
+                add_bias(step)
+            if 0 <= step + 1 < UNITS:
+                first_matmuls(step + 1)
+            if 0 <= step + 4 < len(operands):
+                copy_operand_out(operands[step + 4])
+            if 0 <= step - 1 < UNITS:
+                normalise(step - 1)
+                regroup(step - 1)
+            if 0 <= step - 2 < UNITS:
+                quantise(("p", step - 2), work, "p", p_grouped[step - 2])
+                second_matmuls(step - 2)
+            if 0 <= step < UNITS:
+                row_maxima(step)
+                exponentials(step)
+            if 0 <= step + 5 < len(operands):
+                transpose_operand(operands[step + 5])
+            if 0 <= step - 2 < UNITS:
+                add_residual_and_store(step - 2)
+            if 0 <= step + 4 < len(operands):
+                quantise_operand(operands[step + 4])

@@ -39,9 +39,10 @@ def tile_cmia_pb_t_kernel(
     biases = [b_spa, b_frq]
     outs = [out_0, out_1]
 
-    operands = [("w", 0), ("att", 0), ("w", 1), ("v", 0)]
+    operands = [("w", 0), ("att", 0), ("w", 1)]
     for b in range(1, B):
-        operands.extend([("att", b), ("v", b)])
+        operands.extend([("att", b), ("v", b - 1)])
+    operands.append(("v", B - 1))
 
     with ExitStack() as ctx:
         ctx.enter_context(tc.manual_schedule())
@@ -50,7 +51,7 @@ def tile_cmia_pb_t_kernel(
         late_loads = ctx.enter_context(tc.tile_pool(name="late_loads", bufs=5))
         packed = ctx.enter_context(tc.tile_pool(name="packed", bufs=5))
         work = ctx.enter_context(tc.tile_pool(name="work", bufs=2))
-        soft = ctx.enter_context(tc.tile_pool(name="soft", bufs=3))
+        soft = ctx.enter_context(tc.tile_pool(name="soft", bufs=4))
         stats = ctx.enter_context(tc.tile_pool(name="stats", bufs=4))
         psum_t = ctx.enter_context(tc.psum_pool(name="psum_t", bufs=2))
         psum_z = ctx.enter_context(tc.psum_pool(name="psum_z", bufs=4))
@@ -69,6 +70,7 @@ def tile_cmia_pb_t_kernel(
         probs = {}
         p_grouped = {}
         o_banks = {}
+        results = {}
 
         def load_weight(s):
             rows[("w", s)] = const.tile([P, ROW_TILES * HW], BF16, name="w_rows%d" % s)
@@ -217,17 +219,18 @@ def tile_cmia_pb_t_kernel(
                 )
                 o_banks[unit].append(o)
 
+        def copy_second_half_out(unit):
+            results[unit] = soft.tile([P, C_TILES * HW], F32, name="result")
+            nc.scalar.copy(out=results[unit][:, HW : 2 * HW], in_=o_banks[unit][1][:])
+
         def add_residual_and_store(unit):
             b, s = divmod(unit, 2)
-            result = soft.tile([P, C_TILES * HW], F32, name="result")
-            for ct in range(C_TILES):
-                nc.vector.tensor_tensor(
-                    out=result[:, ct * HW : (ct + 1) * HW],
-                    in0=o_banks[unit][ct][:],
-                    in1=x_rows[b][:, (s * C_TILES + ct) * HW : (s * C_TILES + ct + 1) * HW],
-                    op=ADD,
-                )
-            nc.sync.dma_start(out=outs[s][b].rearrange("(p t) h w -> p (t h w)", t=C_TILES), in_=result[:])
+            x_unit = x_rows[b][:, s * C_TILES * HW : (s + 1) * C_TILES * HW]
+            nc.vector.tensor_tensor(out=results[unit][:, 0:HW], in0=o_banks[unit][0][:], in1=x_unit[:, 0:HW], op=ADD)
+            nc.gpsimd.tensor_tensor(
+                out=results[unit][:, HW : 2 * HW], in0=results[unit][:, HW : 2 * HW], in1=x_unit[:, HW : 2 * HW], op=ADD
+            )
+            nc.sync.dma_start(out=outs[s][b].rearrange("(p t) h w -> p (t h w)", t=C_TILES), in_=results[unit][:])
 
         bias_in = const.tile([P, 2 * HW], BF16, name="bias_in")
         nc.vector.memset(bias_in[:].bitcast(I32), 0)
@@ -245,6 +248,8 @@ def tile_cmia_pb_t_kernel(
             load_att(b)
             load_values_and_residuals(b)
 
+        transpose_operand(operands[0])
+
         bias_rows = []
         for s in range(2):
             spread = psum_z.tile([P, HW], F32, name="z")
@@ -253,7 +258,7 @@ def tile_cmia_pb_t_kernel(
             nc.vector.tensor_copy(out=bias[:], in_=spread[:])
             bias_rows.append(bias)
 
-        for step in range(-5, UNITS + 2):
+        for step in range(-3, UNITS + 2):
             if step >= 0 and step % 2 == 0 and step // 2 + LOAD_AHEAD < B:
                 load_att(step // 2 + LOAD_AHEAD)
                 load_values_and_residuals(step // 2 + LOAD_AHEAD)
@@ -261,20 +266,21 @@ def tile_cmia_pb_t_kernel(
                 add_bias(step)
             if 0 <= step + 1 < UNITS:
                 first_matmuls(step + 1)
-            if 0 <= step + 4 < len(operands):
-                copy_operand_out(operands[step + 4])
+            if step + 3 < len(operands):
+                copy_operand_out(operands[step + 3])
             if 0 <= step - 1 < UNITS:
                 normalise(step - 1)
                 regroup(step - 1)
             if 0 <= step - 2 < UNITS:
                 quantise(("p", step - 2), work, "p", p_grouped[step - 2])
                 second_matmuls(step - 2)
+                copy_second_half_out(step - 2)
             if 0 <= step < UNITS:
                 row_maxima(step)
                 exponentials(step)
-            if 0 <= step + 5 < len(operands):
-                transpose_operand(operands[step + 5])
+            if step + 4 < len(operands):
+                transpose_operand(operands[step + 4])
             if 0 <= step - 2 < UNITS:
                 add_residual_and_store(step - 2)
-            if 0 <= step + 4 < len(operands):
-                quantise_operand(operands[step + 4])
+            if step + 3 < len(operands):
+                quantise_operand(operands[step + 3])

@@ -70,7 +70,6 @@ def tile_cmia_pb_t_kernel(
         probs = {}
         p_grouped = {}
         o_banks = {}
-        results = {}
 
         def load_weight(s):
             rows[("w", s)] = const.tile([P, ROW_TILES * HW], BF16, name="w_rows%d" % s)
@@ -176,19 +175,29 @@ def tile_cmia_pb_t_kernel(
                 )
 
         def normalise(unit):
+            scalar_tiles = ROW_TILES // 2 if unit == UNITS - 1 else ROW_TILES
             inv_sums = stats.tile([P, ROW_TILES], F32, name="inv_sums")
             nc.vector.reciprocal(out=inv_sums[:], in_=sums[unit][:])
             probs[unit] = work.tile([P, ROW_TILES * HW], BF16, name="probs")
             for t in range(ROW_TILES):
-                nc.scalar.activation(
-                    out=probs[unit][:, t * HW : (t + 1) * HW],
-                    in_=logits[unit][:, t * HW : (t + 1) * HW],
-                    func=COPY,
-                    scale=inv_sums[:, t : t + 1],
-                )
+                tile_cols = slice(t * HW, (t + 1) * HW)
+                if t < scalar_tiles:
+                    nc.scalar.activation(
+                        out=probs[unit][:, tile_cols], in_=logits[unit][:, tile_cols], func=COPY, scale=inv_sums[:, t : t + 1]
+                    )
+                else:
+                    nc.vector.tensor_scalar_mul(
+                        out=probs[unit][:, tile_cols], in0=logits[unit][:, tile_cols], scalar1=inv_sums[:, t : t + 1]
+                    )
 
         def regroup(unit):
             p_grouped[unit] = work.tile([P, HW * PACK], BF16, name="p_grouped", align_bytes=64)
+            if unit == UNITS - 1:
+                nc.vector.tensor_copy(
+                    out=p_grouped[unit][:].rearrange("p (c i t) -> p c t i", i=4, t=PACK),
+                    in_=probs[unit][:].rearrange("p (t c i) -> p c t i", t=PACK, i=4),
+                )
+                return
             by_column = probs[unit][:].rearrange("p (t m) -> p m t", t=PACK)
             piece_cols = HW // REGROUP_PIECES
             for piece in range(REGROUP_PIECES):
@@ -219,18 +228,17 @@ def tile_cmia_pb_t_kernel(
                 )
                 o_banks[unit].append(o)
 
-        def copy_second_half_out(unit):
-            results[unit] = soft.tile([P, C_TILES * HW], F32, name="result")
-            nc.scalar.copy(out=results[unit][:, HW : 2 * HW], in_=o_banks[unit][1][:])
-
         def add_residual_and_store(unit):
             b, s = divmod(unit, 2)
-            x_unit = x_rows[b][:, s * C_TILES * HW : (s + 1) * C_TILES * HW]
-            nc.vector.tensor_tensor(out=results[unit][:, 0:HW], in0=o_banks[unit][0][:], in1=x_unit[:, 0:HW], op=ADD)
-            nc.gpsimd.tensor_tensor(
-                out=results[unit][:, HW : 2 * HW], in0=results[unit][:, HW : 2 * HW], in1=x_unit[:, HW : 2 * HW], op=ADD
-            )
-            nc.sync.dma_start(out=outs[s][b].rearrange("(p t) h w -> p (t h w)", t=C_TILES), in_=results[unit][:])
+            result = soft.tile([P, C_TILES * HW], F32, name="result")
+            for ct in range(C_TILES):
+                nc.vector.tensor_tensor(
+                    out=result[:, ct * HW : (ct + 1) * HW],
+                    in0=o_banks[unit][ct][:],
+                    in1=x_rows[b][:, (s * C_TILES + ct) * HW : (s * C_TILES + ct + 1) * HW],
+                    op=ADD,
+                )
+            nc.sync.dma_start(out=outs[s][b].rearrange("(p t) h w -> p (t h w)", t=C_TILES), in_=result[:])
 
         bias_in = const.tile([P, 2 * HW], BF16, name="bias_in")
         nc.vector.memset(bias_in[:].bitcast(I32), 0)
@@ -274,7 +282,8 @@ def tile_cmia_pb_t_kernel(
             if 0 <= step - 2 < UNITS:
                 quantise(("p", step - 2), work, "p", p_grouped[step - 2])
                 second_matmuls(step - 2)
-                copy_second_half_out(step - 2)
+            if step + 3 < len(operands):
+                quantise_operand(operands[step + 3])
             if 0 <= step < UNITS:
                 row_maxima(step)
                 exponentials(step)
@@ -282,5 +291,3 @@ def tile_cmia_pb_t_kernel(
                 transpose_operand(operands[step + 4])
             if 0 <= step - 2 < UNITS:
                 add_residual_and_store(step - 2)
-            if step + 3 < len(operands):
-                quantise_operand(operands[step + 3])

@@ -23,7 +23,6 @@ HW = 512
 ROW_TILES = HW // P
 C_TILES = C // P
 UNITS = 2 * B
-REGROUP_PIECES = 4
 LOAD_AHEAD = 3
 
 FLOPS = 2 * B * 2 * (HW * HW * HW + C * HW * HW)
@@ -198,18 +197,14 @@ def tile_cmia_pb_t_kernel(
                     in_=probs[unit][:].rearrange("p (t c i) -> p c t i", t=PACK, i=4),
                 )
                 return
-            by_column = probs[unit][:].rearrange("p (t m) -> p m t", t=PACK)
-            piece_cols = HW // REGROUP_PIECES
-            for piece in range(REGROUP_PIECES):
-                m0 = piece * piece_cols
-                nc.gpsimd.tensor_scalar(
-                    out=p_grouped[unit][:, m0 * PACK : (m0 + piece_cols) * PACK].rearrange("p (m t) -> p m t", t=PACK),
-                    in0=by_column[:, m0 : m0 + piece_cols, :],
-                    scalar1=1.0,
-                    scalar2=0.0,
-                    op0=MULT,
-                    op1=ADD,
-                )
+            nc.gpsimd.tensor_scalar(
+                out=p_grouped[unit][:].rearrange("p (m t) -> p m t", t=PACK),
+                in0=probs[unit][:].rearrange("p (t m) -> p m t", t=PACK),
+                scalar1=1.0,
+                scalar2=0.0,
+                op0=MULT,
+                op1=ADD,
+            )
 
         def second_matmuls(unit):
             b, s = divmod(unit, 2)
@@ -238,7 +233,10 @@ def tile_cmia_pb_t_kernel(
                     in1=x_rows[b][:, (s * C_TILES + ct) * HW : (s * C_TILES + ct + 1) * HW],
                     op=ADD,
                 )
-            nc.sync.dma_start(out=outs[s][b].rearrange("(p t) h w -> p (t h w)", t=C_TILES), in_=result[:])
+                nc.sync.dma_start(
+                    out=outs[s][b].rearrange("(p t) h w -> p t (h w)", t=C_TILES)[:, ct, :],
+                    in_=result[:, ct * HW : (ct + 1) * HW],
+                )
 
         bias_in = const.tile([P, 2 * HW], BF16, name="bias_in")
         nc.vector.memset(bias_in[:].bitcast(I32), 0)
@@ -266,28 +264,38 @@ def tile_cmia_pb_t_kernel(
             nc.vector.tensor_copy(out=bias[:], in_=spread[:])
             bias_rows.append(bias)
 
-        for step in range(-3, UNITS + 2):
+        for step in range(-3, UNITS):
             if step >= 0 and step % 2 == 0 and step // 2 + LOAD_AHEAD < B:
                 load_att(step // 2 + LOAD_AHEAD)
                 load_values_and_residuals(step // 2 + LOAD_AHEAD)
-            if 0 <= step < UNITS:
+            if step >= 0:
                 add_bias(step)
             if 0 <= step + 1 < UNITS:
                 first_matmuls(step + 1)
             if step + 3 < len(operands):
                 copy_operand_out(operands[step + 3])
-            if 0 <= step - 1 < UNITS:
+            if step >= 1:
                 normalise(step - 1)
                 regroup(step - 1)
-            if 0 <= step - 2 < UNITS:
+            if step >= 2:
                 quantise(("p", step - 2), work, "p", p_grouped[step - 2])
                 second_matmuls(step - 2)
             if step + 3 < len(operands):
                 quantise_operand(operands[step + 3])
-            if 0 <= step < UNITS:
+            if step >= 0:
                 row_maxima(step)
                 exponentials(step)
             if step + 4 < len(operands):
                 transpose_operand(operands[step + 4])
-            if 0 <= step - 2 < UNITS:
+            if step >= 2:
                 add_residual_and_store(step - 2)
+
+        last = UNITS - 1
+        normalise(last)
+        quantise(("p", last - 1), work, "p", p_grouped[last - 1])
+        second_matmuls(last - 1)
+        regroup(last)
+        quantise(("p", last), work, "p", p_grouped[last])
+        second_matmuls(last)
+        add_residual_and_store(last - 1)
+        add_residual_and_store(last)

@@ -14,6 +14,7 @@ MAX = mybir.AluOpType.max
 MULT = mybir.AluOpType.mult
 EXP = mybir.ActivationFunctionType.Exp
 COPY = mybir.ActivationFunctionType.Copy
+IDENTITY = mybir.ActivationFunctionType.Identity
 
 P = 128
 PACK = 4
@@ -50,11 +51,10 @@ def tile_cmia_pb_t_kernel(
         late_loads = ctx.enter_context(tc.tile_pool(name="late_loads", bufs=5))
         packed = ctx.enter_context(tc.tile_pool(name="packed", bufs=5))
         work = ctx.enter_context(tc.tile_pool(name="work", bufs=2))
-        soft = ctx.enter_context(tc.tile_pool(name="soft", bufs=4))
         stats = ctx.enter_context(tc.tile_pool(name="stats", bufs=4))
-        psum_t = ctx.enter_context(tc.psum_pool(name="psum_t", bufs=2))
         psum_z = ctx.enter_context(tc.psum_pool(name="psum_z", bufs=4))
-        psum_o = ctx.enter_context(tc.psum_pool(name="psum_o", bufs=2))
+        psum_y = ctx.enter_context(tc.psum_pool(name="psum_y", bufs=3))
+        psum_o = ctx.enter_context(tc.psum_pool(name="psum_o", bufs=1))
 
         rows = {}
         x_rows = {}
@@ -62,13 +62,17 @@ def tile_cmia_pb_t_kernel(
         grouped = {}
         codes = {}
         scales = {}
-        z_banks = {}
-        logits = {}
+        zt_banks = {}
+        logits_t = {}
+        y_banks = {}
         neg_max = {}
+        exps = {}
         sums = {}
+        inv_sums = {}
         probs = {}
         p_grouped = {}
         o_banks = {}
+        results = {}
 
         def load_weight(s):
             rows[("w", s)] = const.tile([P, ROW_TILES * HW], BF16, name="w_rows%d" % s)
@@ -98,29 +102,49 @@ def tile_cmia_pb_t_kernel(
                     in_=residuals[s][b].rearrange("(p t) h w -> p (t h w)", t=C_TILES),
                 )
 
-        def transpose_operand(op):
+        def transpose_operand(op, half):
             row_words = rows[op][:].bitcast(F32)
-            banks[op] = []
-            for pair in range(2):
-                bank = psum_t.tile([P, 4 * P], F32, name="tr")
-                for j in range(4):
-                    col = (4 * pair + j) * P
-                    nc.tensor.transpose(bank[:, j * P : (j + 1) * P], row_words[:, col : col + P], ident[:])
-                banks[op].append(bank)
+            bank = psum_z.tile([P, 4 * P], F32, name="z")
+            for j in range(4):
+                col = (4 * half + j) * P
+                nc.tensor.transpose(bank[:, j * P : (j + 1) * P], row_words[:, col : col + P], ident[:])
+            banks[(op, half)] = bank
 
-        def copy_operand_out(op):
-            grouped[op] = work.tile([P, HW * PACK], BF16, name="grouped", align_bytes=64)
+        def copy_operand_out(op, half, engine_copy):
+            if half == 0:
+                grouped[op] = work.tile([P, HW * PACK], BF16, name="grouped", align_bytes=64)
             grouped_words = grouped[op][:].bitcast(F32)
-            for pair in range(2):
-                nc.scalar.copy(
-                    out=grouped_words[:, 4 * pair * P : 4 * (pair + 1) * P].rearrange("p (t r u) -> p t r u", t=2, u=2),
-                    in_=banks[op][pair][:].rearrange("p (t u r) -> p t r u", t=2, u=2),
-                )
+            engine_copy(
+                out=grouped_words[:, 4 * half * P : 4 * (half + 1) * P].rearrange("p (t r u) -> p t r u", t=2, u=2),
+                in_=banks[(op, half)][:].rearrange("p (t u r) -> p t r u", t=2, u=2),
+            )
 
         def quantise(key, pool, name, source):
             codes[key] = pool.tile([P, HW], U32, name=name + "_codes", align_bytes=64)
             scales[key] = pool.tile([P, HW], U8, name=name + "_scales", align_bytes=64)
             nc.vector.quantize_mx(out=codes[key][:].bitcast(FP8X4), scales=scales[key][:], in_=source[:])
+
+        def quantise_half(unit, half):
+            key = ("p", unit)
+            if half == 0:
+                codes[key] = work.tile([P, HW], U32, name="p_codes", align_bytes=64)
+                scales[key] = work.tile([P, HW], U8, name="p_scales", align_bytes=64)
+            cols = slice(half * HW // 2, (half + 1) * HW // 2)
+            nc.vector.quantize_mx(
+                out=codes[key][:, cols].bitcast(FP8X4),
+                scales=scales[key][:, cols],
+                in_=p_grouped[unit][:, half * HW * PACK // 2 : (half + 1) * HW * PACK // 2],
+            )
+
+        def regroup_half(unit, half, engine_copy):
+            if half == 0:
+                p_grouped[unit] = work.tile([P, HW * PACK], BF16, name="p_grouped", align_bytes=64)
+            size = HW * PACK // 2
+            source = probs[unit][:].rearrange("p (t h c i) -> p h c t i", t=PACK, h=2, i=4)
+            engine_copy(
+                out=p_grouped[unit][:, half * size : (half + 1) * size].rearrange("p (c i t) -> p c t i", i=4, t=PACK),
+                in_=source[:, half],
+            )
 
         def quantise_operand(op):
             if op[0] == "w":
@@ -128,75 +152,86 @@ def tile_cmia_pb_t_kernel(
             else:
                 quantise(op, packed, "operand", grouped[op])
 
-        def first_matmuls(unit):
+        def first_matmul(unit, j):
             b, s = divmod(unit, 2)
-            z_banks[unit] = []
-            for t in range(ROW_TILES):
-                z = psum_z.tile([P, HW], F32, name="z")
-                nc.tensor.matmul_mx(
-                    out=z[:],
-                    lhsT=codes[("att", b)][:, t * P : (t + 1) * P].bitcast(FP8X4),
-                    lhsT_scale=scales[("att", b)][:, t * P : (t + 1) * P],
-                    rhs=codes[("w", s)][:].bitcast(FP8X4),
-                    rhs_scale=scales[("w", s)][:],
-                    start=True,
-                    stop=True,
-                )
-                z_banks[unit].append(z)
+            zt = psum_z.tile([P, HW], F32, name="z")
+            nc.tensor.matmul_mx(
+                out=zt[:],
+                lhsT=codes[("w", s)][:, j * P : (j + 1) * P].bitcast(FP8X4),
+                lhsT_scale=scales[("w", s)][:, j * P : (j + 1) * P],
+                rhs=codes[("att", b)][:].bitcast(FP8X4),
+                rhs_scale=scales[("att", b)][:],
+                start=True,
+                stop=True,
+            )
+            zt_banks[(unit, j)] = zt
 
-        def add_bias(unit):
-            logits[unit] = soft.tile([P, ROW_TILES * HW], F32, name="logits")
-            for t in range(ROW_TILES):
-                nc.vector.tensor_tensor(
-                    out=logits[unit][:, t * HW : (t + 1) * HW], in0=z_banks[unit][t][:], in1=bias_rows[unit % 2][:], op=ADD
+        def add_bias(unit, j, on_vector=False):
+            if j == 0:
+                logits_t[unit] = work.tile([P, ROW_TILES * HW], F32, name="logits_t")
+            col = (unit % 2) * ROW_TILES + j
+            if on_vector:
+                nc.vector.tensor_scalar_add(
+                    out=logits_t[unit][:, j * HW : (j + 1) * HW],
+                    in0=zt_banks[(unit, j)][:],
+                    scalar1=bias_cols[:, col : col + 1],
                 )
+                return
+            nc.scalar.activation(
+                out=logits_t[unit][:, j * HW : (j + 1) * HW],
+                in_=zt_banks[(unit, j)][:],
+                func=IDENTITY,
+                bias=bias_cols[:, col : col + 1],
+                scale=1.0,
+            )
 
-        def row_maxima(unit):
-            neg_max[unit] = stats.tile([P, ROW_TILES], F32, name="neg_max")
+        def transpose_logits(unit, t):
+            bank = psum_y.tile([P, HW], F32, name="y")
+            for j in range(ROW_TILES):
+                col = j * HW + t * P
+                nc.tensor.transpose(bank[:, j * P : (j + 1) * P], logits_t[unit][:, col : col + P], ident[:])
+            y_banks[(unit, t)] = bank
+
+        def row_max(unit, t):
+            if t == 0:
+                neg_max[unit] = stats.tile([P, ROW_TILES], F32, name="neg_max")
             nc.vector.tensor_reduce(
-                out=neg_max[unit][:],
-                in_=logits[unit][:].rearrange("p (t m) -> p t m", t=ROW_TILES),
+                out=neg_max[unit][:, t : t + 1],
+                in_=y_banks[(unit, t)][:],
                 axis=mybir.AxisListType.X,
                 op=MAX,
                 negate=True,
             )
 
-        def exponentials(unit):
-            sums[unit] = stats.tile([P, ROW_TILES], F32, name="sums")
-            for t in range(ROW_TILES):
-                nc.scalar.activation(
-                    out=logits[unit][:, t * HW : (t + 1) * HW],
-                    in_=logits[unit][:, t * HW : (t + 1) * HW],
-                    func=EXP,
-                    bias=neg_max[unit][:, t : t + 1],
-                    scale=1.0,
-                    accum_out=sums[unit][:, t : t + 1],
-                )
+        def exponential(unit, t):
+            if t == 0:
+                exps[unit] = work.tile([P, ROW_TILES * HW], F32, name="exps")
+                sums[unit] = stats.tile([P, ROW_TILES], F32, name="sums")
+            nc.scalar.activation(
+                out=exps[unit][:, t * HW : (t + 1) * HW],
+                in_=y_banks[(unit, t)][:],
+                func=EXP,
+                bias=neg_max[unit][:, t : t + 1],
+                scale=1.0,
+                accum_out=sums[unit][:, t : t + 1],
+            )
 
-        def normalise(unit):
-            scalar_tiles = ROW_TILES // 2 if unit == UNITS - 1 else ROW_TILES
-            inv_sums = stats.tile([P, ROW_TILES], F32, name="inv_sums")
-            nc.vector.reciprocal(out=inv_sums[:], in_=sums[unit][:])
-            probs[unit] = work.tile([P, ROW_TILES * HW], BF16, name="probs")
-            for t in range(ROW_TILES):
-                tile_cols = slice(t * HW, (t + 1) * HW)
-                if t < scalar_tiles:
-                    nc.scalar.activation(
-                        out=probs[unit][:, tile_cols], in_=logits[unit][:, tile_cols], func=COPY, scale=inv_sums[:, t : t + 1]
-                    )
-                else:
-                    nc.vector.tensor_scalar_mul(
-                        out=probs[unit][:, tile_cols], in0=logits[unit][:, tile_cols], scalar1=inv_sums[:, t : t + 1]
-                    )
+        def invert_sums(unit):
+            inv_sums[unit] = stats.tile([P, ROW_TILES], F32, name="inv_sums")
+            nc.vector.reciprocal(out=inv_sums[unit][:], in_=sums[unit][:])
+
+        def normalise(unit, t, on_scalar=False):
+            if t == 0:
+                probs[unit] = work.tile([P, ROW_TILES * HW], BF16, name="probs")
+            tile_cols = slice(t * HW, (t + 1) * HW)
+            factor = inv_sums[unit][:, t : t + 1]
+            if on_scalar:
+                nc.scalar.activation(out=probs[unit][:, tile_cols], in_=exps[unit][:, tile_cols], func=COPY, scale=factor)
+            else:
+                nc.vector.tensor_scalar_mul(out=probs[unit][:, tile_cols], in0=exps[unit][:, tile_cols], scalar1=factor)
 
         def regroup(unit):
             p_grouped[unit] = work.tile([P, HW * PACK], BF16, name="p_grouped", align_bytes=64)
-            if unit == UNITS - 1:
-                nc.vector.tensor_copy(
-                    out=p_grouped[unit][:].rearrange("p (c i t) -> p c t i", i=4, t=PACK),
-                    in_=probs[unit][:].rearrange("p (t c i) -> p c t i", t=PACK, i=4),
-                )
-                return
             nc.gpsimd.tensor_scalar(
                 out=p_grouped[unit][:].rearrange("p (m t) -> p m t", t=PACK),
                 in0=probs[unit][:].rearrange("p (t m) -> p m t", t=PACK),
@@ -206,96 +241,168 @@ def tile_cmia_pb_t_kernel(
                 op1=ADD,
             )
 
-        def second_matmuls(unit):
+        def second_matmul(unit, ct, pool, name, cols=slice(0, HW)):
             b, s = divmod(unit, 2)
-            o_banks[unit] = []
-            for ct in range(C_TILES):
-                col = (s * C_TILES + ct) * P
-                o = psum_o.tile([P, HW], F32, name="o")
-                nc.tensor.matmul_mx(
-                    out=o[:],
-                    lhsT=codes[("v", b)][:, col : col + P].bitcast(FP8X4),
-                    lhsT_scale=scales[("v", b)][:, col : col + P],
-                    rhs=codes[("p", unit)][:].bitcast(FP8X4),
-                    rhs_scale=scales[("p", unit)][:],
-                    start=True,
-                    stop=True,
-                )
-                o_banks[unit].append(o)
+            col = (s * C_TILES + ct) * P
+            o = pool.tile([P, HW], F32, name=name)
+            nc.tensor.matmul_mx(
+                out=o[:, 0 : cols.stop - cols.start],
+                lhsT=codes[("v", b)][:, col : col + P].bitcast(FP8X4),
+                lhsT_scale=scales[("v", b)][:, col : col + P],
+                rhs=codes[("p", unit)][:, cols].bitcast(FP8X4),
+                rhs_scale=scales[("p", unit)][:, cols],
+                start=True,
+                stop=True,
+            )
+            o_banks[(unit, ct, cols.start)] = o
 
-        def add_residual_and_store(unit):
+        def add_residual_and_store(unit, ct, cols=slice(0, HW)):
             b, s = divmod(unit, 2)
-            result = soft.tile([P, C_TILES * HW], F32, name="result")
-            for ct in range(C_TILES):
-                nc.vector.tensor_tensor(
-                    out=result[:, ct * HW : (ct + 1) * HW],
-                    in0=o_banks[unit][ct][:],
-                    in1=x_rows[b][:, (s * C_TILES + ct) * HW : (s * C_TILES + ct + 1) * HW],
-                    op=ADD,
-                )
-                nc.sync.dma_start(
-                    out=outs[s][b].rearrange("(p t) h w -> p t (h w)", t=C_TILES)[:, ct, :],
-                    in_=result[:, ct * HW : (ct + 1) * HW],
-                )
+            if ct == 0 and cols.start == 0:
+                results[unit] = work.tile([P, C_TILES * HW], F32, name="result", bufs=4)
+            result = results[unit]
+            nc.vector.tensor_tensor(
+                out=result[:, ct * HW + cols.start : ct * HW + cols.stop],
+                in0=o_banks[(unit, ct, cols.start)][:, 0 : cols.stop - cols.start],
+                in1=x_rows[b][:, (s * C_TILES + ct) * HW + cols.start : (s * C_TILES + ct) * HW + cols.stop],
+                op=ADD,
+            )
+            nc.sync.dma_start(
+                out=outs[s][b].rearrange("(p t) h w -> p t (h w)", t=C_TILES)[:, ct, cols],
+                in_=result[:, ct * HW + cols.start : ct * HW + cols.stop],
+            )
 
-        bias_in = const.tile([P, 2 * HW], BF16, name="bias_in")
+        bias_in = const.tile([P, P], BF16, name="bias_in")
         nc.vector.memset(bias_in[:].bitcast(I32), 0)
-        ones = const.tile([P, P], BF16, name="ones")
-        nc.vector.memset(ones[:], 1.0)
         ident = const.tile([P, P], F32, name="ident")
         make_identity(nc, ident[:])
+        ident_bf16 = const.tile([P, P], BF16, name="ident_bf16")
+        nc.vector.tensor_copy(out=ident_bf16[:], in_=ident[:])
         for s in range(2):
-            nc.scalar.dma_start(out=bias_in[0:1, s * HW : (s + 1) * HW], in_=biases[s].unsqueeze(0))
+            nc.scalar.dma_start(
+                out=bias_in[s * ROW_TILES : (s + 1) * ROW_TILES, :], in_=biases[s].rearrange("(j p) -> j p", p=P)
+            )
         load_weight(0)
         load_att(0)
         load_weight(1)
+        load_att(1)
         load_values_and_residuals(0)
-        for b in range(1, LOAD_AHEAD):
-            load_att(b)
-            load_values_and_residuals(b)
+        load_att(2)
+        load_values_and_residuals(1)
+        load_values_and_residuals(2)
 
-        transpose_operand(operands[0])
+        scalar_copy = nc.scalar.copy
+        vector_copy = nc.vector.tensor_copy
 
-        bias_rows = []
-        for s in range(2):
-            spread = psum_z.tile([P, HW], F32, name="z")
-            nc.tensor.matmul(out=spread[:], lhsT=ones[:], rhs=bias_in[:, s * HW : (s + 1) * HW], start=True, stop=True)
-            bias = const.tile([P, HW], F32, name="bias%d" % s)
-            nc.vector.tensor_copy(out=bias[:], in_=spread[:])
-            bias_rows.append(bias)
+        for op in operands[0:2]:
+            transpose_operand(op, 0)
+            transpose_operand(op, 1)
+        for op in operands[0:2]:
+            copy_operand_out(op, 0, scalar_copy)
+            copy_operand_out(op, 1, vector_copy)
+        quantise_operand(operands[0])
+        quantise_operand(operands[1])
 
-        for step in range(-3, UNITS):
-            if step >= 0 and step % 2 == 0 and step // 2 + LOAD_AHEAD < B:
+        bias_bank = psum_y.tile([P, P], BF16, name="y")
+        nc.tensor.transpose(bias_bank[:], bias_in[:], ident_bf16[:])
+        bias_cols = const.tile([P, 2 * ROW_TILES], F32, name="bias_cols")
+        nc.vector.tensor_copy(out=bias_cols[:], in_=bias_bank[:, 0 : 2 * ROW_TILES])
+
+        transpose_operand(operands[2], 0)
+        transpose_operand(operands[2], 1)
+        first_matmul(0, 0)
+        first_matmul(0, 1)
+        copy_operand_out(operands[2], 0, scalar_copy)
+        copy_operand_out(operands[2], 1, vector_copy)
+        add_bias(0, 0)
+        add_bias(0, 1, on_vector=True)
+        first_matmul(0, 2)
+        first_matmul(0, 3)
+        add_bias(0, 2)
+        add_bias(0, 3, on_vector=True)
+        quantise_operand(operands[2])
+        transpose_operand(operands[3], 0)
+        transpose_operand(operands[3], 1)
+        first_matmul(1, 0)
+
+        for step in range(UNITS):
+            op = operands[step + 3] if step + 3 < len(operands) else None
+            next_op = operands[step + 4] if step + 4 < len(operands) else None
+            coming = step + 1 < UNITS
+            done = step >= 1
+            last = step >= 2
+            if step % 2 == 0 and step // 2 + LOAD_AHEAD < B:
                 load_att(step // 2 + LOAD_AHEAD)
                 load_values_and_residuals(step // 2 + LOAD_AHEAD)
-            if step >= 0:
-                add_bias(step)
-            if 0 <= step + 1 < UNITS:
-                first_matmuls(step + 1)
-            if step + 3 < len(operands):
-                copy_operand_out(operands[step + 3])
-            if step >= 1:
-                normalise(step - 1)
+            transpose_logits(step, 0)
+            transpose_logits(step, 1)
+            transpose_logits(step, 2)
+            if op:
+                copy_operand_out(op, 0, scalar_copy)
+            if coming:
+                add_bias(step + 1, 0)
+                first_matmul(step + 1, 1)
+            if op:
+                copy_operand_out(op, 1, scalar_copy)
+            if last:
+                second_matmul(step - 2, 0, psum_o, "o")
+            if done:
+                normalise(step - 1, 0)
+                normalise(step - 1, 1)
+            row_max(step, 0)
+            exponential(step, 0)
+            if done:
+                normalise(step - 1, 2)
+                normalise(step - 1, 3)
                 regroup(step - 1)
-            if step >= 2:
-                quantise(("p", step - 2), work, "p", p_grouped[step - 2])
-                second_matmuls(step - 2)
-            if step + 3 < len(operands):
-                quantise_operand(operands[step + 3])
-            if step >= 0:
-                row_maxima(step)
-                exponentials(step)
-            if step + 4 < len(operands):
-                transpose_operand(operands[step + 4])
-            if step >= 2:
-                add_residual_and_store(step - 2)
+            transpose_logits(step, 3)
+            if coming:
+                add_bias(step + 1, 1)
+            row_max(step, 1)
+            exponential(step, 1)
+            row_max(step, 2)
+            exponential(step, 2)
+            if last:
+                add_residual_and_store(step - 2, 0)
+                second_matmul(step - 2, 1, psum_o, "o")
+            row_max(step, 3)
+            exponential(step, 3)
+            if last:
+                add_residual_and_store(step - 2, 1)
+            if op:
+                quantise_operand(op)
+            invert_sums(step)
+            if coming:
+                first_matmul(step + 1, 2)
+                add_bias(step + 1, 2)
+                first_matmul(step + 1, 3)
+                add_bias(step + 1, 3)
+            if next_op:
+                transpose_operand(next_op, 0)
+                transpose_operand(next_op, 1)
+            if step + 2 < UNITS:
+                first_matmul(step + 2, 0)
+            if done:
+                quantise(("p", step - 1), work, "p", p_grouped[step - 1])
 
         last = UNITS - 1
-        normalise(last)
-        quantise(("p", last - 1), work, "p", p_grouped[last - 1])
-        second_matmuls(last - 1)
-        regroup(last)
-        quantise(("p", last), work, "p", p_grouped[last])
-        second_matmuls(last)
-        add_residual_and_store(last - 1)
-        add_residual_and_store(last)
+        normalise(last, 0)
+        normalise(last, 1)
+        normalise(last, 2, on_scalar=True)
+        normalise(last, 3)
+        second_matmul(last - 1, 0, psum_y, "y")
+        second_matmul(last - 1, 1, psum_y, "y")
+        regroup_half(last, 0, vector_copy)
+        regroup_half(last, 1, scalar_copy)
+        add_residual_and_store(last - 1, 0)
+        quantise_half(last, 0)
+        halves = [slice(0, HW // 2), slice(HW // 2, HW)]
+        for ct in range(C_TILES):
+            second_matmul(last, ct, psum_z, "z", halves[0])
+        add_residual_and_store(last - 1, 1)
+        quantise_half(last, 1)
+        for ct in range(C_TILES):
+            second_matmul(last, ct, psum_z, "z", halves[1])
+        for cols in halves:
+            for ct in range(C_TILES):
+                add_residual_and_store(last, ct, cols)

@@ -187,6 +187,8 @@ def tile_cmia_pb_t_kernel(
 
         def transpose_logits(unit, t):
             bank = psum_y.tile([P, HW], F32, name="y")
+            if t % 2 == 1:
+                nc.tensor.matmul(out=bank[:], lhsT=ident_bf16[:], rhs=busy_rows[:], start=True, stop=True)
             for j in range(ROW_TILES):
                 col = j * HW + t * P
                 nc.tensor.transpose(bank[:, j * P : (j + 1) * P], logits_t[unit][:, col : col + P], ident[:])
@@ -276,6 +278,8 @@ def tile_cmia_pb_t_kernel(
         nc.vector.memset(bias_in[:].bitcast(I32), 0)
         ident = const.tile([P, P], F32, name="ident")
         make_identity(nc, ident[:])
+        busy_rows = const.tile([P, HW], BF16, name="busy_rows")
+        nc.vector.memset(busy_rows[:].bitcast(I32), 0)
         ident_bf16 = const.tile([P, P], BF16, name="ident_bf16")
         nc.vector.tensor_copy(out=ident_bf16[:], in_=ident[:])
         for s in range(2):

@@ -47,13 +47,13 @@ def tile_cmia_pb_t_kernel(
     with ExitStack() as ctx:
         ctx.enter_context(tc.manual_schedule())
         const = ctx.enter_context(tc.tile_pool(name="const", bufs=1))
-        loads = ctx.enter_context(tc.tile_pool(name="loads", bufs=3))
+        loads = ctx.enter_context(tc.tile_pool(name="loads", bufs=4))
         late_loads = ctx.enter_context(tc.tile_pool(name="late_loads", bufs=5))
-        packed = ctx.enter_context(tc.tile_pool(name="packed", bufs=5))
+        packed = ctx.enter_context(tc.tile_pool(name="packed", bufs=6))
         work = ctx.enter_context(tc.tile_pool(name="work", bufs=2))
         stats = ctx.enter_context(tc.tile_pool(name="stats", bufs=4))
-        psum_z = ctx.enter_context(tc.psum_pool(name="psum_z", bufs=4))
-        psum_y = ctx.enter_context(tc.psum_pool(name="psum_y", bufs=3))
+        psum_z = ctx.enter_context(tc.psum_pool(name="psum_z", bufs=3))
+        psum_y = ctx.enter_context(tc.psum_pool(name="psum_y", bufs=4))
         psum_o = ctx.enter_context(tc.psum_pool(name="psum_o", bufs=1))
 
         rows = {}
@@ -88,23 +88,28 @@ def tile_cmia_pb_t_kernel(
                 in_=att[b].rearrange("(u p e) k -> p u e k", u=2, e=2),
             )
 
-        def load_values_and_residuals(b):
+        def load_values(b):
             rows[("v", b)] = loads.tile([P, 2 * C_TILES * HW], BF16, name="v_rows")
-            x_rows[b] = late_loads.tile([P, 2 * C_TILES * HW], BF16, name="x_rows")
             for s in range(2):
                 nc.sync.dma_start(
                     out=rows[("v", b)][:, s * C_TILES * HW : (s + 1) * C_TILES * HW],
                     in_=values[s][b].rearrange("(p t) n -> p (t n)", t=C_TILES),
                 )
+
+        def load_residuals(b):
+            x_rows[b] = late_loads.tile([P, 2 * C_TILES * HW], BF16, name="x_rows")
             for s in range(2):
                 nc.sync.dma_start(
                     out=x_rows[b][:, s * C_TILES * HW : (s + 1) * C_TILES * HW],
                     in_=residuals[s][b].rearrange("(p t) h w -> p (t h w)", t=C_TILES),
                 )
 
-        def transpose_operand(op, half):
+        def transpose_operand(op, half, in_head=False):
             row_words = rows[op][:].bitcast(F32)
-            bank = psum_z.tile([P, 4 * P], F32, name="z")
+            if in_head and half == 1:
+                bank = psum_y.tile([P, 4 * P], F32, name="y")
+            else:
+                bank = psum_z.tile([P, 4 * P], F32, name="z")
             for j in range(4):
                 col = (4 * half + j) * P
                 nc.tensor.transpose(bank[:, j * P : (j + 1) * P], row_words[:, col : col + P], ident[:])
@@ -112,7 +117,7 @@ def tile_cmia_pb_t_kernel(
 
         def copy_operand_out(op, half, engine_copy):
             if half == 0:
-                grouped[op] = work.tile([P, HW * PACK], BF16, name="grouped", align_bytes=64)
+                grouped[op] = work.tile([P, HW * PACK], BF16, name="grouped", bufs=3, align_bytes=64)
             grouped_words = grouped[op][:].bitcast(F32)
             engine_copy(
                 out=grouped_words[:, 4 * half * P : 4 * (half + 1) * P].rearrange("p (t r u) -> p t r u", t=2, u=2),
@@ -136,14 +141,15 @@ def tile_cmia_pb_t_kernel(
                 in_=p_grouped[unit][:, half * HW * PACK // 2 : (half + 1) * HW * PACK // 2],
             )
 
-        def regroup_half(unit, half, engine_copy):
-            if half == 0:
+        def regroup_part(unit, first, count, engine_copy):
+            if first == 0:
                 p_grouped[unit] = work.tile([P, HW * PACK], BF16, name="p_grouped", align_bytes=64)
-            size = HW * PACK // 2
-            source = probs[unit][:].rearrange("p (t h c i) -> p h c t i", t=PACK, h=2, i=4)
+            size = HW * PACK // 4
+            groups = HW // 4 // 4
+            source = probs[unit][:].rearrange("p (t c i) -> p c t i", t=PACK, i=4)
             engine_copy(
-                out=p_grouped[unit][:, half * size : (half + 1) * size].rearrange("p (c i t) -> p c t i", i=4, t=PACK),
-                in_=source[:, half],
+                out=p_grouped[unit][:, first * size : (first + count) * size].rearrange("p (c i t) -> p c t i", i=4, t=PACK),
+                in_=source[:, first * groups : (first + count) * groups],
             )
 
         def quantise_operand(op):
@@ -187,8 +193,6 @@ def tile_cmia_pb_t_kernel(
 
         def transpose_logits(unit, t):
             bank = psum_y.tile([P, HW], F32, name="y")
-            if t % 2 == 1:
-                nc.tensor.matmul(out=bank[:], lhsT=ident_bf16[:], rhs=busy_rows[:], start=True, stop=True)
             for j in range(ROW_TILES):
                 col = j * HW + t * P
                 nc.tensor.transpose(bank[:, j * P : (j + 1) * P], logits_t[unit][:, col : col + P], ident[:])
@@ -278,8 +282,6 @@ def tile_cmia_pb_t_kernel(
         nc.vector.memset(bias_in[:].bitcast(I32), 0)
         ident = const.tile([P, P], F32, name="ident")
         make_identity(nc, ident[:])
-        busy_rows = const.tile([P, HW], BF16, name="busy_rows")
-        nc.vector.memset(busy_rows[:].bitcast(I32), 0)
         ident_bf16 = const.tile([P, P], BF16, name="ident_bf16")
         nc.vector.tensor_copy(out=ident_bf16[:], in_=ident[:])
         for s in range(2):
@@ -290,17 +292,20 @@ def tile_cmia_pb_t_kernel(
         load_att(0)
         load_weight(1)
         load_att(1)
-        load_values_and_residuals(0)
+        load_values(0)
         load_att(2)
-        load_values_and_residuals(1)
-        load_values_and_residuals(2)
+        load_values(1)
+        load_residuals(0)
+        load_values(2)
+        load_residuals(1)
+        load_residuals(2)
 
         scalar_copy = nc.scalar.copy
         vector_copy = nc.vector.tensor_copy
 
         for op in operands[0:2]:
-            transpose_operand(op, 0)
-            transpose_operand(op, 1)
+            transpose_operand(op, 0, in_head=True)
+            transpose_operand(op, 1, in_head=True)
         for op in operands[0:2]:
             copy_operand_out(op, 0, scalar_copy)
             copy_operand_out(op, 1, vector_copy)
@@ -312,101 +317,127 @@ def tile_cmia_pb_t_kernel(
         bias_cols = const.tile([P, 2 * ROW_TILES], F32, name="bias_cols")
         nc.vector.tensor_copy(out=bias_cols[:], in_=bias_bank[:, 0 : 2 * ROW_TILES])
 
-        transpose_operand(operands[2], 0)
-        transpose_operand(operands[2], 1)
-        first_matmul(0, 0)
-        first_matmul(0, 1)
+        transpose_operand(operands[2], 0, in_head=True)
+        transpose_operand(operands[2], 1, in_head=True)
         copy_operand_out(operands[2], 0, scalar_copy)
-        copy_operand_out(operands[2], 1, vector_copy)
-        add_bias(0, 0)
-        add_bias(0, 1, on_vector=True)
-        first_matmul(0, 2)
-        first_matmul(0, 3)
-        add_bias(0, 2)
-        add_bias(0, 3, on_vector=True)
+        copy_operand_out(operands[2], 1, scalar_copy)
+        for j in range(ROW_TILES):
+            first_matmul(0, j)
+            add_bias(0, j, on_vector=j % 2 == 1)
         quantise_operand(operands[2])
         transpose_operand(operands[3], 0)
+        copy_operand_out(operands[3], 0, scalar_copy)
+        for t in range(ROW_TILES):
+            transpose_logits(0, t)
         transpose_operand(operands[3], 1)
+        for t in range(ROW_TILES):
+            row_max(0, t)
+            exponential(0, t)
         first_matmul(1, 0)
+        first_matmul(1, 1)
+        copy_operand_out(operands[3], 1, vector_copy)
+        add_bias(1, 0, on_vector=True)
+        first_matmul(1, 2)
+        add_bias(1, 1)
+        first_matmul(1, 3)
+        add_bias(1, 2, on_vector=True)
+        transpose_operand(operands[4], 0)
+        add_bias(1, 3)
+        transpose_operand(operands[4], 1)
+        for t in range(ROW_TILES):
+            transpose_logits(1, t)
+        quantise_operand(operands[3])
+        copy_operand_out(operands[4], 0, scalar_copy)
+        transpose_operand(operands[5], 0)
+        copy_operand_out(operands[4], 1, scalar_copy)
+        first_matmul(2, 0)
+        transpose_operand(operands[5], 1)
 
-        for step in range(UNITS):
-            op = operands[step + 3] if step + 3 < len(operands) else None
-            next_op = operands[step + 4] if step + 4 < len(operands) else None
+        for step in range(1, UNITS):
+            op = operands[step + 4] if step + 4 < len(operands) else None
+            next_op = operands[step + 5] if step + 5 < len(operands) else None
             coming = step + 1 < UNITS
-            done = step >= 1
             last = step >= 2
-            if step % 2 == 0 and step // 2 + LOAD_AHEAD < B:
+            if step % 2 == 1 and step // 2 + LOAD_AHEAD < B:
                 load_att(step // 2 + LOAD_AHEAD)
-                load_values_and_residuals(step // 2 + LOAD_AHEAD)
-            transpose_logits(step, 0)
-            transpose_logits(step, 1)
-            transpose_logits(step, 2)
+                load_values(step // 2 + LOAD_AHEAD)
+                load_residuals(step // 2 + LOAD_AHEAD)
+            if last and step + 3 < len(operands):
+                quantise_operand(operands[step + 3])
+            invert_sums(step - 1)
+            if last:
+                quantise(("p", step - 2), work, "p", p_grouped[step - 2])
+            for t in range(ROW_TILES):
+                normalise(step - 1, t, on_scalar=not coming and t < 2)
+            regroup(step - 1)
+            if not last:
+                quantise_operand(operands[step + 3])
             if op:
                 copy_operand_out(op, 0, scalar_copy)
             if coming:
-                add_bias(step + 1, 0)
                 first_matmul(step + 1, 1)
-            if op:
-                copy_operand_out(op, 1, scalar_copy)
+                add_bias(step + 1, 0)
+                first_matmul(step + 1, 2)
             if last:
                 second_matmul(step - 2, 0, psum_o, "o")
-            if done:
-                normalise(step - 1, 0)
-                normalise(step - 1, 1)
+            if op:
+                copy_operand_out(op, 1, scalar_copy)
+            if coming:
+                first_matmul(step + 1, 3)
+                add_bias(step + 1, 1)
+            if next_op:
+                transpose_operand(next_op, 0)
+            if coming:
+                add_bias(step + 1, 2)
+            if step + 2 < UNITS:
+                first_matmul(step + 2, 0)
+            if coming:
+                add_bias(step + 1, 3)
+            if next_op:
+                transpose_operand(next_op, 1)
             row_max(step, 0)
             exponential(step, 0)
-            if done:
-                normalise(step - 1, 2)
-                normalise(step - 1, 3)
-                regroup(step - 1)
-            transpose_logits(step, 3)
             if coming:
-                add_bias(step + 1, 1)
+                transpose_logits(step + 1, 0)
             row_max(step, 1)
             exponential(step, 1)
-            row_max(step, 2)
-            exponential(step, 2)
             if last:
                 add_residual_and_store(step - 2, 0)
                 second_matmul(step - 2, 1, psum_o, "o")
+            if coming:
+                transpose_logits(step + 1, 1)
+            row_max(step, 2)
+            exponential(step, 2)
+            if coming:
+                transpose_logits(step + 1, 2)
             row_max(step, 3)
             exponential(step, 3)
+            if coming:
+                transpose_logits(step + 1, 3)
             if last:
                 add_residual_and_store(step - 2, 1)
-            if op:
-                quantise_operand(op)
-            invert_sums(step)
-            if coming:
-                first_matmul(step + 1, 2)
-                add_bias(step + 1, 2)
-                first_matmul(step + 1, 3)
-                add_bias(step + 1, 3)
-            if next_op:
-                transpose_operand(next_op, 0)
-                transpose_operand(next_op, 1)
-            if step + 2 < UNITS:
-                first_matmul(step + 2, 0)
-            if done:
-                quantise(("p", step - 1), work, "p", p_grouped[step - 1])
 
         last = UNITS - 1
+        quantise(("p", last - 1), work, "p", p_grouped[last - 1])
+        invert_sums(last)
         normalise(last, 0)
         normalise(last, 1)
         normalise(last, 2, on_scalar=True)
         normalise(last, 3)
         second_matmul(last - 1, 0, psum_y, "y")
         second_matmul(last - 1, 1, psum_y, "y")
-        regroup_half(last, 0, vector_copy)
-        regroup_half(last, 1, scalar_copy)
-        add_residual_and_store(last - 1, 0)
+        regroup_part(last, 0, 2, vector_copy)
+        regroup_part(last, 3, 1, scalar_copy)
+        regroup_part(last, 2, 1, vector_copy)
         quantise_half(last, 0)
         halves = [slice(0, HW // 2), slice(HW // 2, HW)]
         for ct in range(C_TILES):
             second_matmul(last, ct, psum_z, "z", halves[0])
-        add_residual_and_store(last - 1, 1)
         quantise_half(last, 1)
         for ct in range(C_TILES):
             second_matmul(last, ct, psum_z, "z", halves[1])
+        add_residual_and_store(last - 1, 0)
+        add_residual_and_store(last - 1, 1)
         for cols in halves:
             for ct in range(C_TILES):
                 add_residual_and_store(last, ct, cols)

@@ -74,11 +74,12 @@ def tile_cmia_pb_t_kernel(
         o_banks = {}
         results = {}
 
-        def load_weight(s):
-            rows[("w", s)] = const.tile([P, ROW_TILES * HW], BF16, name="w_rows%d" % s)
+        def load_weight(s, first, count):
+            if first == 0:
+                rows[("w", s)] = const.tile([P, ROW_TILES * HW], BF16, name="w_rows%d" % s)
             nc.sync.dma_start(
-                out=rows[("w", s)][:].rearrange("p (t k) -> p t k", t=ROW_TILES),
-                in_=weights[s].rearrange("(t p) k -> p t k", p=P),
+                out=rows[("w", s)][:, first * HW : (first + count) * HW].rearrange("p (t k) -> p t k", t=count),
+                in_=weights[s].rearrange("(t p) k -> p t k", p=P)[:, first : first + count, :],
             )
 
         def load_att(b):
@@ -129,16 +130,15 @@ def tile_cmia_pb_t_kernel(
             scales[key] = pool.tile([P, HW], U8, name=name + "_scales", align_bytes=64)
             nc.vector.quantize_mx(out=codes[key][:].bitcast(FP8X4), scales=scales[key][:], in_=source[:])
 
-        def quantise_half(unit, half):
-            key = ("p", unit)
+        def quantise_half(key, pool, name, source, half):
             if half == 0:
-                codes[key] = work.tile([P, HW], U32, name="p_codes", align_bytes=64)
-                scales[key] = work.tile([P, HW], U8, name="p_scales", align_bytes=64)
+                codes[key] = pool.tile([P, HW], U32, name=name + "_codes", align_bytes=64)
+                scales[key] = pool.tile([P, HW], U8, name=name + "_scales", align_bytes=64)
             cols = slice(half * HW // 2, (half + 1) * HW // 2)
             nc.vector.quantize_mx(
                 out=codes[key][:, cols].bitcast(FP8X4),
                 scales=scales[key][:, cols],
-                in_=p_grouped[unit][:, half * HW * PACK // 2 : (half + 1) * HW * PACK // 2],
+                in_=source[:, half * HW * PACK // 2 : (half + 1) * HW * PACK // 2],
             )
 
         def regroup_part(unit, first, count, engine_copy):
@@ -158,9 +158,9 @@ def tile_cmia_pb_t_kernel(
             else:
                 quantise(op, packed, "operand", grouped[op])
 
-        def first_matmul(unit, j):
+        def first_matmul(unit, j, pool=psum_z, name="z"):
             b, s = divmod(unit, 2)
-            zt = psum_z.tile([P, HW], F32, name="z")
+            zt = pool.tile([P, HW], F32, name=name)
             nc.tensor.matmul_mx(
                 out=zt[:],
                 lhsT=codes[("w", s)][:, j * P : (j + 1) * P].bitcast(FP8X4),
@@ -190,6 +190,9 @@ def tile_cmia_pb_t_kernel(
                 bias=bias_cols[:, col : col + 1],
                 scale=1.0,
             )
+
+        def vector_bias(step):
+            return step > 0
 
         def transpose_logits(unit, t):
             bank = psum_y.tile([P, HW], F32, name="y")
@@ -288,9 +291,10 @@ def tile_cmia_pb_t_kernel(
             nc.scalar.dma_start(
                 out=bias_in[s * ROW_TILES : (s + 1) * ROW_TILES, :], in_=biases[s].rearrange("(j p) -> j p", p=P)
             )
-        load_weight(0)
+        load_weight(0, 0, 2)
         load_att(0)
-        load_weight(1)
+        load_weight(0, 2, 2)
+        load_weight(1, 0, 4)
         load_att(1)
         load_values(0)
         load_att(2)
@@ -303,14 +307,18 @@ def tile_cmia_pb_t_kernel(
         scalar_copy = nc.scalar.copy
         vector_copy = nc.vector.tensor_copy
 
-        for op in operands[0:2]:
-            transpose_operand(op, 0, in_head=True)
-            transpose_operand(op, 1, in_head=True)
-        for op in operands[0:2]:
-            copy_operand_out(op, 0, scalar_copy)
-            copy_operand_out(op, 1, vector_copy)
-        quantise_operand(operands[0])
-        quantise_operand(operands[1])
+        w0, att0 = operands[0:2]
+        transpose_operand(w0, 0, in_head=True)
+        transpose_operand(att0, 0, in_head=True)
+        transpose_operand(att0, 1, in_head=True)
+        transpose_operand(w0, 1, in_head=True)
+        copy_operand_out(w0, 0, scalar_copy)
+        copy_operand_out(att0, 0, scalar_copy)
+        quantise_half(w0, const, "w0", grouped[w0], 0)
+        copy_operand_out(att0, 1, vector_copy)
+        copy_operand_out(w0, 1, scalar_copy)
+        quantise_operand(att0)
+        quantise_half(w0, const, "w0", grouped[w0], 1)
 
         bias_bank = psum_y.tile([P, P], BF16, name="y")
         nc.tensor.transpose(bias_bank[:], bias_in[:], ident_bf16[:])
@@ -320,17 +328,26 @@ def tile_cmia_pb_t_kernel(
         transpose_operand(operands[2], 0, in_head=True)
         transpose_operand(operands[2], 1, in_head=True)
         copy_operand_out(operands[2], 0, scalar_copy)
+        first_matmul(0, 0)
+        first_matmul(0, 1)
+        first_matmul(0, 2)
+        first_matmul(0, 3, psum_o, "o")
+        add_bias(0, 0)
+        add_bias(0, 1, on_vector=True)
+        add_bias(0, 2)
+        add_bias(0, 3, on_vector=True)
         copy_operand_out(operands[2], 1, scalar_copy)
-        for j in range(ROW_TILES):
-            first_matmul(0, j)
-            add_bias(0, j, on_vector=j % 2 == 1)
-        quantise_operand(operands[2])
-        transpose_operand(operands[3], 0)
-        copy_operand_out(operands[3], 0, scalar_copy)
         for t in range(ROW_TILES):
             transpose_logits(0, t)
+        row_max(0, 0)
+        exponential(0, 0)
+        quantise_operand(operands[2])
+        row_max(0, 1)
+        exponential(0, 1)
+        transpose_operand(operands[3], 0)
+        copy_operand_out(operands[3], 0, scalar_copy)
         transpose_operand(operands[3], 1)
-        for t in range(ROW_TILES):
+        for t in range(2, ROW_TILES):
             row_max(0, t)
             exponential(0, t)
         first_matmul(1, 0)
@@ -377,6 +394,9 @@ def tile_cmia_pb_t_kernel(
             if coming:
                 first_matmul(step + 1, 1)
                 add_bias(step + 1, 0)
+            if step > 1:
+                transpose_logits(step, 2)
+            if coming:
                 first_matmul(step + 1, 2)
             if last:
                 second_matmul(step - 2, 0, psum_o, "o")
@@ -385,55 +405,59 @@ def tile_cmia_pb_t_kernel(
             if coming:
                 first_matmul(step + 1, 3)
                 add_bias(step + 1, 1)
+            if step > 1:
+                transpose_logits(step, 3)
             if next_op:
                 transpose_operand(next_op, 0)
             if coming:
                 add_bias(step + 1, 2)
             if step + 2 < UNITS:
                 first_matmul(step + 2, 0)
-            if coming:
+            if coming and not vector_bias(step):
                 add_bias(step + 1, 3)
-            if next_op:
-                transpose_operand(next_op, 1)
+                if next_op:
+                    transpose_operand(next_op, 1)
             row_max(step, 0)
             exponential(step, 0)
-            if coming:
-                transpose_logits(step + 1, 0)
             row_max(step, 1)
             exponential(step, 1)
-            if last:
+            row_max(step, 2)
+            if last and coming:
                 add_residual_and_store(step - 2, 0)
                 second_matmul(step - 2, 1, psum_o, "o")
-            if coming:
-                transpose_logits(step + 1, 1)
-            row_max(step, 2)
             exponential(step, 2)
-            if coming:
-                transpose_logits(step + 1, 2)
             row_max(step, 3)
             exponential(step, 3)
             if coming:
-                transpose_logits(step + 1, 3)
+                if vector_bias(step):
+                    add_bias(step + 1, 3, on_vector=True)
+                    if next_op:
+                        transpose_operand(next_op, 1)
+                transpose_logits(step + 1, 0)
+                transpose_logits(step + 1, 1)
+            if last and not coming:
+                add_residual_and_store(step - 2, 0)
+                second_matmul(step - 2, 1, psum_z, "z")
             if last:
                 add_residual_and_store(step - 2, 1)
 
         last = UNITS - 1
-        quantise(("p", last - 1), work, "p", p_grouped[last - 1])
         invert_sums(last)
         normalise(last, 0)
         normalise(last, 1)
         normalise(last, 2, on_scalar=True)
         normalise(last, 3)
+        quantise(("p", last - 1), work, "p", p_grouped[last - 1])
         second_matmul(last - 1, 0, psum_y, "y")
         second_matmul(last - 1, 1, psum_y, "y")
         regroup_part(last, 0, 2, vector_copy)
         regroup_part(last, 3, 1, scalar_copy)
         regroup_part(last, 2, 1, vector_copy)
-        quantise_half(last, 0)
+        quantise_half(("p", last), work, "p", p_grouped[last], 0)
         halves = [slice(0, HW // 2), slice(HW // 2, HW)]
         for ct in range(C_TILES):
             second_matmul(last, ct, psum_z, "z", halves[0])
-        quantise_half(last, 1)
+        quantise_half(("p", last), work, "p", p_grouped[last], 1)
         for ct in range(C_TILES):
             second_matmul(last, ct, psum_z, "z", halves[1])
         add_residual_and_store(last - 1, 0)

@@ -116,6 +116,14 @@ def tile_cmia_pb_t_kernel(
                 nc.tensor.transpose(bank[:, j * P : (j + 1) * P], row_words[:, col : col + P], ident[:])
             banks[(op, half)] = bank
 
+        def keep_busy(bank, count=1):
+            for i in range(count):
+                nc.tensor.matmul(out=bank[:, 0:P], lhsT=ident[:], rhs=ident[:], start=True, stop=True)
+
+        def open_logits_bank(unit, t):
+            y_banks[(unit, t)] = psum_y.tile([P, HW], F32, name="y")
+            keep_busy(y_banks[(unit, t)])
+
         def copy_operand_out(op, half, engine_copy):
             if half == 0:
                 grouped[op] = work.tile([P, HW * PACK], BF16, name="grouped", bufs=3, align_bytes=64)
@@ -191,15 +199,13 @@ def tile_cmia_pb_t_kernel(
                 scale=1.0,
             )
 
-        def vector_bias(step):
-            return step > 0
-
         def transpose_logits(unit, t):
-            bank = psum_y.tile([P, HW], F32, name="y")
+            if (unit, t) not in y_banks:
+                y_banks[(unit, t)] = psum_y.tile([P, HW], F32, name="y")
+            bank = y_banks[(unit, t)]
             for j in range(ROW_TILES):
                 col = j * HW + t * P
                 nc.tensor.transpose(bank[:, j * P : (j + 1) * P], logits_t[unit][:, col : col + P], ident[:])
-            y_banks[(unit, t)] = bank
 
         def row_max(unit, t):
             if t == 0:
@@ -307,11 +313,15 @@ def tile_cmia_pb_t_kernel(
         scalar_copy = nc.scalar.copy
         vector_copy = nc.vector.tensor_copy
 
+        idle_bank = psum_o.tile([P, HW], F32, name="o")
+        keep_busy(idle_bank, 4)
         w0, att0 = operands[0:2]
         transpose_operand(w0, 0, in_head=True)
+        keep_busy(idle_bank, 2)
         transpose_operand(att0, 0, in_head=True)
         transpose_operand(att0, 1, in_head=True)
         transpose_operand(w0, 1, in_head=True)
+        keep_busy(idle_bank, 2)
         copy_operand_out(w0, 0, scalar_copy)
         copy_operand_out(att0, 0, scalar_copy)
         quantise_half(w0, const, "w0", grouped[w0], 0)
@@ -338,6 +348,7 @@ def tile_cmia_pb_t_kernel(
         add_bias(0, 3, on_vector=True)
         copy_operand_out(operands[2], 1, scalar_copy)
         for t in range(ROW_TILES):
+            open_logits_bank(0, t)
             transpose_logits(0, t)
         row_max(0, 0)
         exponential(0, 0)
@@ -398,43 +409,43 @@ def tile_cmia_pb_t_kernel(
                 transpose_logits(step, 2)
             if coming:
                 first_matmul(step + 1, 2)
-            if last:
-                second_matmul(step - 2, 0, psum_o, "o")
+            if step > 1:
+                transpose_logits(step, 3)
             if op:
                 copy_operand_out(op, 1, scalar_copy)
             if coming:
                 first_matmul(step + 1, 3)
+            if last:
+                second_matmul(step - 2, 0, psum_o, "o")
+            if coming:
                 add_bias(step + 1, 1)
-            if step > 1:
-                transpose_logits(step, 3)
             if next_op:
                 transpose_operand(next_op, 0)
             if coming:
                 add_bias(step + 1, 2)
             if step + 2 < UNITS:
                 first_matmul(step + 2, 0)
-            if coming and not vector_bias(step):
+            if coming:
                 add_bias(step + 1, 3)
-                if next_op:
-                    transpose_operand(next_op, 1)
+            if next_op:
+                transpose_operand(next_op, 1)
             row_max(step, 0)
             exponential(step, 0)
             row_max(step, 1)
             exponential(step, 1)
-            row_max(step, 2)
             if last and coming:
                 add_residual_and_store(step - 2, 0)
                 second_matmul(step - 2, 1, psum_o, "o")
+            if coming:
+                transpose_logits(step + 1, 0)
+                open_logits_bank(step + 1, 1)
+                transpose_logits(step + 1, 1)
+            row_max(step, 2)
             exponential(step, 2)
+            if coming:
+                open_logits_bank(step + 1, 2)
             row_max(step, 3)
             exponential(step, 3)
-            if coming:
-                if vector_bias(step):
-                    add_bias(step + 1, 3, on_vector=True)
-                    if next_op:
-                        transpose_operand(next_op, 1)
-                transpose_logits(step + 1, 0)
-                transpose_logits(step + 1, 1)
             if last and not coming:
                 add_residual_and_store(step - 2, 0)
                 second_matmul(step - 2, 1, psum_z, "z")

@@ -105,12 +105,14 @@ def tile_cmia_pb_t_kernel(
                     in_=residuals[s][b].rearrange("(p t) h w -> p (t h w)", t=C_TILES),
                 )
 
-        def transpose_operand(op, half, in_head=False):
+        def transpose_operand(op, half, in_head=False, busy=False):
             row_words = rows[op][:].bitcast(F32)
             if in_head and half == 1:
                 bank = psum_y.tile([P, 4 * P], F32, name="y")
             else:
                 bank = psum_z.tile([P, 4 * P], F32, name="z")
+            if busy:
+                keep_busy(bank)
             for j in range(4):
                 col = (4 * half + j) * P
                 nc.tensor.transpose(bank[:, j * P : (j + 1) * P], row_words[:, col : col + P], ident[:])
@@ -409,18 +411,18 @@ def tile_cmia_pb_t_kernel(
                 transpose_logits(step, 2)
             if coming:
                 first_matmul(step + 1, 2)
-            if step > 1:
-                transpose_logits(step, 3)
             if op:
                 copy_operand_out(op, 1, scalar_copy)
             if coming:
                 first_matmul(step + 1, 3)
             if last:
                 second_matmul(step - 2, 0, psum_o, "o")
+            if step > 1:
+                transpose_logits(step, 3)
             if coming:
                 add_bias(step + 1, 1)
             if next_op:
-                transpose_operand(next_op, 0)
+                transpose_operand(next_op, 0, busy=True)
             if coming:
                 add_bias(step + 1, 2)
             if step + 2 < UNITS:

@@ -354,9 +354,9 @@ def tile_cmia_pb_t_kernel(
             transpose_logits(0, t)
         row_max(0, 0)
         exponential(0, 0)
-        quantise_operand(operands[2])
         row_max(0, 1)
         exponential(0, 1)
+        quantise_operand(operands[2])
         transpose_operand(operands[3], 0)
         copy_operand_out(operands[3], 0, scalar_copy)
         transpose_operand(operands[3], 1)
@@ -375,6 +375,8 @@ def tile_cmia_pb_t_kernel(
         add_bias(1, 3)
         transpose_operand(operands[4], 1)
         for t in range(ROW_TILES):
+            if t % 2 == 1:
+                open_logits_bank(1, t)
             transpose_logits(1, t)
         quantise_operand(operands[3])
         copy_operand_out(operands[4], 0, scalar_copy)
@@ -388,6 +390,8 @@ def tile_cmia_pb_t_kernel(
             next_op = operands[step + 5] if step + 5 < len(operands) else None
             coming = step + 1 < UNITS
             last = step >= 2
+            early = step == 1
+            late = step >= UNITS - 2
             if step % 2 == 1 and step // 2 + LOAD_AHEAD < B:
                 load_att(step // 2 + LOAD_AHEAD)
                 load_values(step // 2 + LOAD_AHEAD)
@@ -423,34 +427,44 @@ def tile_cmia_pb_t_kernel(
                 add_bias(step + 1, 1)
             if next_op:
                 transpose_operand(next_op, 0, busy=True)
-            if coming:
+            if coming and not early:
                 add_bias(step + 1, 2)
-            if step + 2 < UNITS:
+            if step + 2 < UNITS and not early:
                 first_matmul(step + 2, 0)
-            if coming:
+            if coming and not early:
                 add_bias(step + 1, 3)
-            if next_op:
+            if next_op and not early:
                 transpose_operand(next_op, 1)
+            if late:
+                second_matmul(step - 2, 1, psum_z, "z")
             row_max(step, 0)
             exponential(step, 0)
             row_max(step, 1)
             exponential(step, 1)
-            if last and coming:
+            if last and not late:
                 add_residual_and_store(step - 2, 0)
                 second_matmul(step - 2, 1, psum_o, "o")
+            if early:
+                row_max(step, 2)
+                row_max(step, 3)
+                add_bias(step + 1, 2, on_vector=True)
+                first_matmul(step + 2, 0)
+                add_bias(step + 1, 3, on_vector=True)
+                transpose_operand(next_op, 1)
             if coming:
                 transpose_logits(step + 1, 0)
                 open_logits_bank(step + 1, 1)
                 transpose_logits(step + 1, 1)
-            row_max(step, 2)
+            if not early:
+                row_max(step, 2)
             exponential(step, 2)
             if coming:
                 open_logits_bank(step + 1, 2)
-            row_max(step, 3)
+            if not early:
+                row_max(step, 3)
             exponential(step, 3)
-            if last and not coming:
+            if late:
                 add_residual_and_store(step - 2, 0)
-                second_matmul(step - 2, 1, psum_z, "z")
             if last:
                 add_residual_and_store(step - 2, 1)
 
@@ -459,21 +473,20 @@ def tile_cmia_pb_t_kernel(
         normalise(last, 0)
         normalise(last, 1)
         normalise(last, 2, on_scalar=True)
-        normalise(last, 3)
+        normalise(last, 3, on_scalar=True)
         quantise(("p", last - 1), work, "p", p_grouped[last - 1])
         second_matmul(last - 1, 0, psum_y, "y")
         second_matmul(last - 1, 1, psum_y, "y")
         regroup_part(last, 0, 2, vector_copy)
-        regroup_part(last, 3, 1, scalar_copy)
-        regroup_part(last, 2, 1, vector_copy)
+        regroup_part(last, 2, 2, scalar_copy)
+        add_residual_and_store(last - 1, 0)
         quantise_half(("p", last), work, "p", p_grouped[last], 0)
         halves = [slice(0, HW // 2), slice(HW // 2, HW)]
         for ct in range(C_TILES):
             second_matmul(last, ct, psum_z, "z", halves[0])
         quantise_half(("p", last), work, "p", p_grouped[last], 1)
         for ct in range(C_TILES):
-            second_matmul(last, ct, psum_z, "z", halves[1])
-        add_residual_and_store(last - 1, 0)
+            second_matmul(last, ct, psum_y, "y", halves[1])
         add_residual_and_store(last - 1, 1)
         for cols in halves:
             for ct in range(C_TILES):

@@ -182,20 +182,20 @@ def tile_cmia_pb_t_kernel(
             )
             zt_banks[(unit, j)] = zt
 
-        def add_bias(unit, j, on_vector=False):
+        def add_bias(unit, j, on_vector=False, cols=slice(0, HW)):
             if j == 0:
                 logits_t[unit] = work.tile([P, ROW_TILES * HW], F32, name="logits_t")
             col = (unit % 2) * ROW_TILES + j
             if on_vector:
                 nc.vector.tensor_scalar_add(
-                    out=logits_t[unit][:, j * HW : (j + 1) * HW],
-                    in0=zt_banks[(unit, j)][:],
+                    out=logits_t[unit][:, j * HW + cols.start : j * HW + cols.stop],
+                    in0=zt_banks[(unit, j)][:, cols],
                     scalar1=bias_cols[:, col : col + 1],
                 )
                 return
             nc.scalar.activation(
-                out=logits_t[unit][:, j * HW : (j + 1) * HW],
-                in_=zt_banks[(unit, j)][:],
+                out=logits_t[unit][:, j * HW + cols.start : j * HW + cols.stop],
+                in_=zt_banks[(unit, j)][:, cols],
                 func=IDENTITY,
                 bias=bias_cols[:, col : col + 1],
                 scale=1.0,
@@ -237,12 +237,21 @@ def tile_cmia_pb_t_kernel(
             inv_sums[unit] = stats.tile([P, ROW_TILES], F32, name="inv_sums")
             nc.vector.reciprocal(out=inv_sums[unit][:], in_=sums[unit][:])
 
-        def normalise(unit, t, on_scalar=False):
+        def normalise(unit, t, on_scalar=False, on_gpsimd=False):
             if t == 0:
                 probs[unit] = work.tile([P, ROW_TILES * HW], BF16, name="probs")
             tile_cols = slice(t * HW, (t + 1) * HW)
             factor = inv_sums[unit][:, t : t + 1]
-            if on_scalar:
+            if on_gpsimd:
+                nc.gpsimd.tensor_scalar(
+                    out=probs[unit][:, tile_cols],
+                    in0=exps[unit][:, tile_cols],
+                    scalar1=factor,
+                    scalar2=0.0,
+                    op0=MULT,
+                    op1=ADD,
+                )
+            elif on_scalar:
                 nc.scalar.activation(out=probs[unit][:, tile_cols], in_=exps[unit][:, tile_cols], func=COPY, scale=factor)
             else:
                 nc.vector.tensor_scalar_mul(out=probs[unit][:, tile_cols], in0=exps[unit][:, tile_cols], scalar1=factor)
@@ -402,7 +411,7 @@ def tile_cmia_pb_t_kernel(
             if last:
                 quantise(("p", step - 2), work, "p", p_grouped[step - 2])
             for t in range(ROW_TILES):
-                normalise(step - 1, t, on_scalar=not coming and t < 2)
+                normalise(step - 1, t, on_scalar=not coming and t < 2, on_gpsimd=t == 3 and not late and not early)
             regroup(step - 1)
             if not last:
                 quantise_operand(operands[step + 3])
@@ -432,9 +441,10 @@ def tile_cmia_pb_t_kernel(
             if step + 2 < UNITS and not early:
                 first_matmul(step + 2, 0)
             if coming and not early:
-                add_bias(step + 1, 3)
-            if next_op and not early:
-                transpose_operand(next_op, 1)
+                if late:
+                    add_bias(step + 1, 3)
+                else:
+                    add_bias(step + 1, 3, cols=slice(0, HW // 2))
             if late:
                 second_matmul(step - 2, 1, psum_z, "z")
             row_max(step, 0)
@@ -463,6 +473,10 @@ def tile_cmia_pb_t_kernel(
             if not early:
                 row_max(step, 3)
             exponential(step, 3)
+            if coming and not early and not late:
+                add_bias(step + 1, 3, on_vector=True, cols=slice(HW // 2, HW))
+                if next_op:
+                    transpose_operand(next_op, 1)
             if late:
                 add_residual_and_store(step - 2, 0)
             if last:

@@ -383,16 +383,17 @@ def tile_cmia_pb_t_kernel(
         transpose_operand(operands[4], 0)
         add_bias(1, 3)
         transpose_operand(operands[4], 1)
-        for t in range(ROW_TILES):
-            if t % 2 == 1:
-                open_logits_bank(1, t)
-            transpose_logits(1, t)
         quantise_operand(operands[3])
+        transpose_logits(1, 0)
         copy_operand_out(operands[4], 0, scalar_copy)
-        transpose_operand(operands[5], 0)
+        transpose_operand(operands[5], 0, busy=True)
+        transpose_logits(1, 1)
         copy_operand_out(operands[4], 1, scalar_copy)
         first_matmul(2, 0)
+        transpose_logits(1, 2)
         transpose_operand(operands[5], 1)
+        open_logits_bank(1, 3)
+        transpose_logits(1, 3)
 
         for step in range(1, UNITS):
             op = operands[step + 4] if step + 4 < len(operands) else None
@@ -444,7 +445,7 @@ def tile_cmia_pb_t_kernel(
                 if late:
                     add_bias(step + 1, 3)
                 else:
-                    add_bias(step + 1, 3, cols=slice(0, HW // 2))
+                    add_bias(step + 1, 3, cols=slice(0, 3 * P))
             if late:
                 second_matmul(step - 2, 1, psum_z, "z")
             row_max(step, 0)
@@ -474,7 +475,7 @@ def tile_cmia_pb_t_kernel(
                 row_max(step, 3)
             exponential(step, 3)
             if coming and not early and not late:
-                add_bias(step + 1, 3, on_vector=True, cols=slice(HW // 2, HW))
+                add_bias(step + 1, 3, on_vector=True, cols=slice(3 * P, HW))
                 if next_op:
                     transpose_operand(next_op, 1)
             if late:

from contextlib import ExitStack

import concourse.mybir as mybir
from concourse.masks import make_identity

F32 = mybir.dt.float32
BF16 = mybir.dt.bfloat16
I32 = mybir.dt.int32
U32 = mybir.dt.uint32
U8 = mybir.dt.uint8
FP8X4 = mybir.dt.float8_e4m3fn_x4
ADD = mybir.AluOpType.add
MAX = mybir.AluOpType.max
MULT = mybir.AluOpType.mult
EXP = mybir.ActivationFunctionType.Exp
COPY = mybir.ActivationFunctionType.Copy
IDENTITY = mybir.ActivationFunctionType.Identity

P = 128
PACK = 4
B = 8
C = 256
HW = 512
ROW_TILES = HW // P
C_TILES = C // P
UNITS = 2 * B
LOAD_AHEAD = 3

FLOPS = 2 * B * 2 * (HW * HW * HW + C * HW * HW)


def tile_cmia_pb_t_kernel(
    tc, att, v_spa, v_freq, x_spa, x_freq, w_spa, b_spa, w_frq, b_frq, out_0, out_1
):
    nc = tc.nc
    values = [v_spa, v_freq]
    residuals = [x_spa, x_freq]
    weights = [w_spa, w_frq]
    biases = [b_spa, b_frq]
    outs = [out_0, out_1]

    operands = [("w", 0), ("att", 0), ("w", 1)]
    for b in range(1, B):
        operands.extend([("att", b), ("v", b - 1)])
    operands.append(("v", B - 1))

    with ExitStack() as ctx:
        ctx.enter_context(tc.manual_schedule())
        const = ctx.enter_context(tc.tile_pool(name="const", bufs=1))
        loads = ctx.enter_context(tc.tile_pool(name="loads", bufs=4))
        late_loads = ctx.enter_context(tc.tile_pool(name="late_loads", bufs=5))
        packed = ctx.enter_context(tc.tile_pool(name="packed", bufs=6))
        work = ctx.enter_context(tc.tile_pool(name="work", bufs=2))
        stats = ctx.enter_context(tc.tile_pool(name="stats", bufs=4))
        psum_z = ctx.enter_context(tc.psum_pool(name="psum_z", bufs=3))
        psum_y = ctx.enter_context(tc.psum_pool(name="psum_y", bufs=4))
        psum_o = ctx.enter_context(tc.psum_pool(name="psum_o", bufs=1))

        rows = {}
        x_rows = {}
        banks = {}
        grouped = {}
        codes = {}
        scales = {}
        zt_banks = {}
        logits_t = {}
        y_banks = {}
        neg_max = {}
        exps = {}
        sums = {}
        inv_sums = {}
        probs = {}
        p_grouped = {}
        o_banks = {}
        results = {}

        def load_weight(s, first, count):
            if first == 0:
                rows[("w", s)] = const.tile([P, ROW_TILES * HW], BF16, name="w_rows%d" % s)
            nc.sync.dma_start(
                out=rows[("w", s)][:, first * HW : (first + count) * HW].rearrange("p (t k) -> p t k", t=count),
                in_=weights[s].rearrange("(t p) k -> p t k", p=P)[:, first : first + count, :],
            )

        def load_att(b):
            rows[("att", b)] = loads.tile([P, ROW_TILES * HW], BF16, name="att_rows")
            nc.sync.dma_start(
                out=rows[("att", b)][:].rearrange("p (u e k) -> p u e k", u=2, e=2),
                in_=att[b].rearrange("(u p e) k -> p u e k", u=2, e=2),
            )

        def load_values(b):
            rows[("v", b)] = loads.tile([P, 2 * C_TILES * HW], BF16, name="v_rows")
            for s in range(2):
                nc.sync.dma_start(
                    out=rows[("v", b)][:, s * C_TILES * HW : (s + 1) * C_TILES * HW],
                    in_=values[s][b].rearrange("(p t) n -> p (t n)", t=C_TILES),
                )

        def load_residuals(b):
            x_rows[b] = late_loads.tile([P, 2 * C_TILES * HW], BF16, name="x_rows")
            for s in range(2):
                nc.sync.dma_start(
                    out=x_rows[b][:, s * C_TILES * HW : (s + 1) * C_TILES * HW],
                    in_=residuals[s][b].rearrange("(p t) h w -> p (t h w)", t=C_TILES),
                )

        def transpose_operand(op, half, in_head=False, busy=False):
            row_words = rows[op][:].bitcast(F32)
            if in_head and half == 1:
                bank = psum_y.tile([P, 4 * P], F32, name="y")
            else:
                bank = psum_z.tile([P, 4 * P], F32, name="z")
            if busy:
                keep_busy(bank)
            for j in range(4):
                col = (4 * half + j) * P
                nc.tensor.transpose(bank[:, j * P : (j + 1) * P], row_words[:, col : col + P], ident[:])
            banks[(op, half)] = bank

        def keep_busy(bank, count=1):
            for i in range(count):
                nc.tensor.matmul(out=bank[:, 0:P], lhsT=ident[:], rhs=ident[:], start=True, stop=True)

        def open_logits_bank(unit, t):
            y_banks[(unit, t)] = psum_y.tile([P, HW], F32, name="y")
            keep_busy(y_banks[(unit, t)])

        def copy_operand_out(op, half, engine_copy):
            if half == 0:
                grouped[op] = work.tile([P, HW * PACK], BF16, name="grouped", bufs=3, align_bytes=64)
            grouped_words = grouped[op][:].bitcast(F32)
            engine_copy(
                out=grouped_words[:, 4 * half * P : 4 * (half + 1) * P].rearrange("p (t r u) -> p t r u", t=2, u=2),
                in_=banks[(op, half)][:].rearrange("p (t u r) -> p t r u", t=2, u=2),
            )

        def quantise(key, pool, name, source):
            codes[key] = pool.tile([P, HW], U32, name=name + "_codes", align_bytes=64)
            scales[key] = pool.tile([P, HW], U8, name=name + "_scales", align_bytes=64)
            nc.vector.quantize_mx(out=codes[key][:].bitcast(FP8X4), scales=scales[key][:], in_=source[:])

        def quantise_half(key, pool, name, source, half):
            if half == 0:
                codes[key] = pool.tile([P, HW], U32, name=name + "_codes", align_bytes=64)
                scales[key] = pool.tile([P, HW], U8, name=name + "_scales", align_bytes=64)
            cols = slice(half * HW // 2, (half + 1) * HW // 2)
            nc.vector.quantize_mx(
                out=codes[key][:, cols].bitcast(FP8X4),
                scales=scales[key][:, cols],
                in_=source[:, half * HW * PACK // 2 : (half + 1) * HW * PACK // 2],
            )

        def regroup_part(unit, first, count, engine_copy):
            if first == 0:
                p_grouped[unit] = work.tile([P, HW * PACK], BF16, name="p_grouped", align_bytes=64)
            size = HW * PACK // 4
            groups = HW // 4 // 4
            source = probs[unit][:].rearrange("p (t c i) -> p c t i", t=PACK, i=4)
            engine_copy(
                out=p_grouped[unit][:, first * size : (first + count) * size].rearrange("p (c i t) -> p c t i", i=4, t=PACK),
                in_=source[:, first * groups : (first + count) * groups],
            )

        def quantise_operand(op):
            if op[0] == "w":
                quantise(op, const, "w%d" % op[1], grouped[op])
            else:
                quantise(op, packed, "operand", grouped[op])

        def first_matmul(unit, j, pool=psum_z, name="z"):
            b, s = divmod(unit, 2)
            zt = pool.tile([P, HW], F32, name=name)
            nc.tensor.matmul_mx(
                out=zt[:],
                lhsT=codes[("w", s)][:, j * P : (j + 1) * P].bitcast(FP8X4),
                lhsT_scale=scales[("w", s)][:, j * P : (j + 1) * P],
                rhs=codes[("att", b)][:].bitcast(FP8X4),
                rhs_scale=scales[("att", b)][:],
                start=True,
                stop=True,
            )
            zt_banks[(unit, j)] = zt

        def add_bias(unit, j, on_vector=False, cols=slice(0, HW)):
            if j == 0:
                logits_t[unit] = work.tile([P, ROW_TILES * HW], F32, name="logits_t")
            col = (unit % 2) * ROW_TILES + j
            if on_vector:
                nc.vector.tensor_scalar_add(
                    out=logits_t[unit][:, j * HW + cols.start : j * HW + cols.stop],
                    in0=zt_banks[(unit, j)][:, cols],
                    scalar1=bias_cols[:, col : col + 1],
                )
                return
            nc.scalar.activation(
                out=logits_t[unit][:, j * HW + cols.start : j * HW + cols.stop],
                in_=zt_banks[(unit, j)][:, cols],
                func=IDENTITY,
                bias=bias_cols[:, col : col + 1],
                scale=1.0,
            )

        def transpose_logits(unit, t):
            if (unit, t) not in y_banks:
                y_banks[(unit, t)] = psum_y.tile([P, HW], F32, name="y")
            bank = y_banks[(unit, t)]
            for j in range(ROW_TILES):
                col = j * HW + t * P
                nc.tensor.transpose(bank[:, j * P : (j + 1) * P], logits_t[unit][:, col : col + P], ident[:])

        def row_max(unit, t):
            if t == 0:
                neg_max[unit] = stats.tile([P, ROW_TILES], F32, name="neg_max")
            nc.vector.tensor_reduce(
                out=neg_max[unit][:, t : t + 1],
                in_=y_banks[(unit, t)][:],
                axis=mybir.AxisListType.X,
                op=MAX,
                negate=True,
            )

        def exponential(unit, t):
            if t == 0:
                exps[unit] = work.tile([P, ROW_TILES * HW], F32, name="exps")
                sums[unit] = stats.tile([P, ROW_TILES], F32, name="sums")
            nc.scalar.activation(
                out=exps[unit][:, t * HW : (t + 1) * HW],
                in_=y_banks[(unit, t)][:],
                func=EXP,
                bias=neg_max[unit][:, t : t + 1],
                scale=1.0,
                accum_out=sums[unit][:, t : t + 1],
            )

        def invert_sums(unit):
            inv_sums[unit] = stats.tile([P, ROW_TILES], F32, name="inv_sums")
            nc.vector.reciprocal(out=inv_sums[unit][:], in_=sums[unit][:])

        def normalise(unit, t, on_scalar=False, on_gpsimd=False):
            if t == 0:
                probs[unit] = work.tile([P, ROW_TILES * HW], BF16, name="probs")
            tile_cols = slice(t * HW, (t + 1) * HW)
            factor = inv_sums[unit][:, t : t + 1]
            if on_gpsimd:
                nc.gpsimd.tensor_scalar(
                    out=probs[unit][:, tile_cols],
                    in0=exps[unit][:, tile_cols],
                    scalar1=factor,
                    scalar2=0.0,
                    op0=MULT,
                    op1=ADD,
                )
            elif on_scalar:
                nc.scalar.activation(out=probs[unit][:, tile_cols], in_=exps[unit][:, tile_cols], func=COPY, scale=factor)
            else:
                nc.vector.tensor_scalar_mul(out=probs[unit][:, tile_cols], in0=exps[unit][:, tile_cols], scalar1=factor)

        def regroup(unit):
            p_grouped[unit] = work.tile([P, HW * PACK], BF16, name="p_grouped", align_bytes=64)
            nc.gpsimd.tensor_scalar(
                out=p_grouped[unit][:].rearrange("p (m t) -> p m t", t=PACK),
                in0=probs[unit][:].rearrange("p (t m) -> p m t", t=PACK),
                scalar1=1.0,
                scalar2=0.0,
                op0=MULT,
                op1=ADD,
            )

        def second_matmul(unit, ct, pool, name, cols=slice(0, HW)):
            b, s = divmod(unit, 2)
            col = (s * C_TILES + ct) * P
            o = pool.tile([P, HW], F32, name=name)
            nc.tensor.matmul_mx(
                out=o[:, 0 : cols.stop - cols.start],
                lhsT=codes[("v", b)][:, col : col + P].bitcast(FP8X4),
                lhsT_scale=scales[("v", b)][:, col : col + P],
                rhs=codes[("p", unit)][:, cols].bitcast(FP8X4),
                rhs_scale=scales[("p", unit)][:, cols],
                start=True,
                stop=True,
            )
            o_banks[(unit, ct, cols.start)] = o

        def add_residual_and_store(unit, ct, cols=slice(0, HW)):
            b, s = divmod(unit, 2)
            if ct == 0 and cols.start == 0:
                results[unit] = work.tile([P, C_TILES * HW], F32, name="result", bufs=4)
            result = results[unit]
            nc.vector.tensor_tensor(
                out=result[:, ct * HW + cols.start : ct * HW + cols.stop],
                in0=o_banks[(unit, ct, cols.start)][:, 0 : cols.stop - cols.start],
                in1=x_rows[b][:, (s * C_TILES + ct) * HW + cols.start : (s * C_TILES + ct) * HW + cols.stop],
                op=ADD,
            )
            nc.sync.dma_start(
                out=outs[s][b].rearrange("(p t) h w -> p t (h w)", t=C_TILES)[:, ct, cols],
                in_=result[:, ct * HW + cols.start : ct * HW + cols.stop],
            )

        bias_in = const.tile([P, P], BF16, name="bias_in")
        nc.vector.memset(bias_in[:].bitcast(I32), 0)
        ident = const.tile([P, P], F32, name="ident")
        make_identity(nc, ident[:])
        ident_bf16 = const.tile([P, P], BF16, name="ident_bf16")
        nc.vector.tensor_copy(out=ident_bf16[:], in_=ident[:])
        for s in range(2):
            nc.scalar.dma_start(
                out=bias_in[s * ROW_TILES : (s + 1) * ROW_TILES, :], in_=biases[s].rearrange("(j p) -> j p", p=P)
            )
        load_weight(0, 0, 2)
        load_att(0)
        load_weight(0, 2, 2)
        load_weight(1, 0, 4)
        load_att(1)
        load_values(0)
        load_att(2)
        load_values(1)
        load_residuals(0)
        load_values(2)
        load_residuals(1)
        load_residuals(2)

        scalar_copy = nc.scalar.copy
        vector_copy = nc.vector.tensor_copy

        idle_bank = psum_o.tile([P, HW], F32, name="o")
        keep_busy(idle_bank, 4)
        w0, att0 = operands[0:2]
        transpose_operand(w0, 0, in_head=True)
        keep_busy(idle_bank, 2)
        transpose_operand(att0, 0, in_head=True)
        transpose_operand(att0, 1, in_head=True)
        transpose_operand(w0, 1, in_head=True)
        keep_busy(idle_bank, 2)
        copy_operand_out(w0, 0, scalar_copy)
        copy_operand_out(att0, 0, scalar_copy)
        quantise_half(w0, const, "w0", grouped[w0], 0)
        copy_operand_out(att0, 1, vector_copy)
        copy_operand_out(w0, 1, scalar_copy)
        quantise_operand(att0)
        quantise_half(w0, const, "w0", grouped[w0], 1)

        bias_bank = psum_y.tile([P, P], BF16, name="y")
        nc.tensor.transpose(bias_bank[:], bias_in[:], ident_bf16[:])
        bias_cols = const.tile([P, 2 * ROW_TILES], F32, name="bias_cols")
        nc.vector.tensor_copy(out=bias_cols[:], in_=bias_bank[:, 0 : 2 * ROW_TILES])

        transpose_operand(operands[2], 0, in_head=True)
        transpose_operand(operands[2], 1, in_head=True)
        copy_operand_out(operands[2], 0, scalar_copy)
        first_matmul(0, 0)
        first_matmul(0, 1)
        first_matmul(0, 2)
        first_matmul(0, 3, psum_o, "o")
        add_bias(0, 0)
        add_bias(0, 1, on_vector=True)
        add_bias(0, 2)
        add_bias(0, 3, on_vector=True)
        copy_operand_out(operands[2], 1, scalar_copy)
        for t in range(ROW_TILES):
            open_logits_bank(0, t)
            transpose_logits(0, t)
        row_max(0, 0)
        exponential(0, 0)
        row_max(0, 1)
        exponential(0, 1)
        quantise_operand(operands[2])
        transpose_operand(operands[3], 0)
        copy_operand_out(operands[3], 0, scalar_copy)
        transpose_operand(operands[3], 1)
        for t in range(2, ROW_TILES):
            row_max(0, t)
            exponential(0, t)
        first_matmul(1, 0)
        first_matmul(1, 1)
        copy_operand_out(operands[3], 1, vector_copy)
        add_bias(1, 0, on_vector=True)
        first_matmul(1, 2)
        add_bias(1, 1)
        first_matmul(1, 3)
        add_bias(1, 2, on_vector=True)
        transpose_operand(operands[4], 0)
        add_bias(1, 3)
        transpose_operand(operands[4], 1)
        quantise_operand(operands[3])
        transpose_logits(1, 0)
        copy_operand_out(operands[4], 0, scalar_copy)
        transpose_operand(operands[5], 0, busy=True)
        transpose_logits(1, 1)
        copy_operand_out(operands[4], 1, scalar_copy)
        first_matmul(2, 0)
        transpose_logits(1, 2)
        transpose_operand(operands[5], 1)
        open_logits_bank(1, 3)
        transpose_logits(1, 3)

        for step in range(1, UNITS):
            op = operands[step + 4] if step + 4 < len(operands) else None
            next_op = operands[step + 5] if step + 5 < len(operands) else None
            coming = step + 1 < UNITS
            last = step >= 2
            early = step == 1
            late = step >= UNITS - 2
            if step % 2 == 1 and step // 2 + LOAD_AHEAD < B:
                load_att(step // 2 + LOAD_AHEAD)
                load_values(step // 2 + LOAD_AHEAD)
                load_residuals(step // 2 + LOAD_AHEAD)
            if last and step + 3 < len(operands):
                quantise_operand(operands[step + 3])
            invert_sums(step - 1)
            if last:
                quantise(("p", step - 2), work, "p", p_grouped[step - 2])
            for t in range(ROW_TILES):
                normalise(step - 1, t, on_scalar=not coming and t < 2, on_gpsimd=t == 3 and not late and not early)
            regroup(step - 1)
            if not last:
                quantise_operand(operands[step + 3])
            if op:
                copy_operand_out(op, 0, scalar_copy)
            if coming:
                first_matmul(step + 1, 1)
                add_bias(step + 1, 0)
            if step > 1:
                transpose_logits(step, 2)
            if coming:
                first_matmul(step + 1, 2)
            if op:
                copy_operand_out(op, 1, scalar_copy)
            if coming:
                first_matmul(step + 1, 3)
            if last:
                second_matmul(step - 2, 0, psum_o, "o")
            if step > 1:
                transpose_logits(step, 3)
            if coming:
                add_bias(step + 1, 1)
            if next_op:
                transpose_operand(next_op, 0, busy=True)
            if coming and not early:
                add_bias(step + 1, 2)
            if step + 2 < UNITS and not early:
                first_matmul(step + 2, 0)
            if coming and not early:
                if late:
                    add_bias(step + 1, 3)
                else:
                    add_bias(step + 1, 3, cols=slice(0, 3 * P))
            if late:
                second_matmul(step - 2, 1, psum_z, "z")
            row_max(step, 0)
            exponential(step, 0)
            row_max(step, 1)
            exponential(step, 1)
            if last and not late:
                add_residual_and_store(step - 2, 0)
                second_matmul(step - 2, 1, psum_o, "o")
            if early:
                row_max(step, 2)
                row_max(step, 3)
                add_bias(step + 1, 2, on_vector=True)
                first_matmul(step + 2, 0)
                add_bias(step + 1, 3, on_vector=True)
                transpose_operand(next_op, 1)
            if coming:
                transpose_logits(step + 1, 0)
                open_logits_bank(step + 1, 1)
                transpose_logits(step + 1, 1)
            if not early:
                row_max(step, 2)
            exponential(step, 2)
            if coming:
                open_logits_bank(step + 1, 2)
            if not early:
                row_max(step, 3)
            exponential(step, 3)
            if coming and not early and not late:
                add_bias(step + 1, 3, on_vector=True, cols=slice(3 * P, HW))
                if next_op:
                    transpose_operand(next_op, 1)
            if late:
                add_residual_and_store(step - 2, 0)
            if last:
                add_residual_and_store(step - 2, 1)

        last = UNITS - 1
        invert_sums(last)
        normalise(last, 0)
        normalise(last, 1)
        normalise(last, 2, on_scalar=True)
        normalise(last, 3, on_scalar=True)
        quantise(("p", last - 1), work, "p", p_grouped[last - 1])
        second_matmul(last - 1, 0, psum_y, "y")
        second_matmul(last - 1, 1, psum_y, "y")
        regroup_part(last, 0, 2, vector_copy)
        regroup_part(last, 2, 2, scalar_copy)
        add_residual_and_store(last - 1, 0)
        quantise_half(("p", last), work, "p", p_grouped[last], 0)
        halves = [slice(0, HW // 2), slice(HW // 2, HW)]
        for ct in range(C_TILES):
            second_matmul(last, ct, psum_z, "z", halves[0])
        quantise_half(("p", last), work, "p", p_grouped[last], 1)
        for ct in range(C_TILES):
            second_matmul(last, ct, psum_y, "y", halves[1])
        add_residual_and_store(last - 1, 1)
        for cols in halves:
            for ct in range(C_TILES):
                add_residual_and_store(last, ct, cols)
